import numpy as np
import ml_dtypes


def mxq(x, axis, fmt="e4m3"):
    dtype, down = {"e4m3": (ml_dtypes.float8_e4m3fn, 7), "e5m2": (ml_dtypes.float8_e5m2, 14)}[fmt]
    v = np.moveaxis(np.asarray(x, np.float32).astype(ml_dtypes.bfloat16).astype(np.float64), axis, -1)
    blocks = v.reshape(v.shape[:-1] + (-1, 32))
    amax = np.abs(blocks).max(-1, keepdims=True)
    byte = np.maximum(np.where(amax > 0, np.frexp(amax)[1] - 1 + 127, 0) - down, 1)
    scale = np.exp2(byte - 127.0)
    codes = (blocks / scale).astype(np.float32).astype(dtype).astype(np.float64)
    return np.moveaxis((codes * scale).reshape(v.shape), -1, axis)


WIDE = False


def mx_kscale(k):
    if not WIDE:
        return np.ones(k)
    levels = np.array([10, -10, 5, -5, 0])
    a = np.random.permutation(np.resize(levels, k // 512 * 4)).reshape(k // 512, 4)
    idx = np.arange(k)
    return np.exp2(a[idx // 512, idx % 128 // 32])


BF16 = ml_dtypes.bfloat16


def bf(x):
    return np.asarray(x, np.float32).astype(BF16)


def f64(x):
    return np.asarray(x).astype(np.float64)


E2M1 = np.array([0.0, 0.5, 1.0, 1.5, 2.0, 3.0, 4.0, 6.0, -0.0, -0.5, -1.0, -1.5, -2.0, -3.0, -4.0, -6.0])


def pack_weight(w, fmt):
    k, n = w.shape
    w = f64(bf(w)).reshape(k // 32, 32, n)
    amax = np.abs(w).max(1)
    if fmt == "e4m3":
        byte = np.frexp(amax)[1] - 1 + 127 - 7
    else:
        mant, ex = np.frexp(amax / 6.0)
        byte = np.where(mant > 0.5, ex, ex - 1) + 127
    byte = np.clip(np.where(amax > 0, byte, 1), 1, 254)
    scaled = (w * np.exp2(127.0 - byte)[:, None, :]).reshape(k, n).astype(np.float32)
    by_word = np.ascontiguousarray(scaled.reshape(k // 512, 128, 4, n).transpose(0, 1, 3, 2))
    if fmt == "e4m3":
        words = by_word.astype(ml_dtypes.float8_e4m3fn).view(np.uint8)
    else:
        c = by_word.astype(ml_dtypes.float4_e2m1fn).view(np.uint8) & 0xF
        words = c[..., 0::2] | (c[..., 1::2] << 4)
    return np.ascontiguousarray(words), np.ascontiguousarray(byte.astype(np.uint8).reshape(k // 512, 16, n))


def unpack_weight(words, scales, fmt):
    g, p, n, _ = words.shape
    if fmt == "e4m3":
        vals = np.ascontiguousarray(words).view(ml_dtypes.float8_e4m3fn).astype(np.float64)
    else:
        nib = np.empty((g, p, n, 4), np.uint8)
        nib[..., 0::2] = words & 0xF
        nib[..., 1::2] = words >> 4
        vals = E2M1[nib]
    vals = vals * np.repeat(np.exp2(scales.astype(np.float64) - 127.0), 8, axis=1)[..., None]
    return vals.transpose(0, 1, 3, 2).reshape(g * 512, n)


B, C, H, W = 2, 512, 32, 24
N = H * W
EPS = 1e-5
XS = np.sqrt((np.log(C) + 2.0) / N)
FMT = "e4m3"


def setup_inputs():
    s = mx_kscale(C)
    s = s / s.max()
    x = bf(np.random.standard_normal((B, C, H, W)) * XS * s[None, :, None, None])
    conv_w = np.random.standard_normal((C, C)) / (XS * np.sqrt(C)) / s[None, :]
    words, scales = pack_weight(np.ascontiguousarray(conv_w.T), FMT)
    gamma = bf(1.0 + 0.1 * np.random.standard_normal(C))
    beta = bf(0.1 * np.random.standard_normal(C))
    return {"x": x,
            "conv_w_words": words,
            "conv_w_scales": scales,
            "gamma": gamma,
            "beta": beta}


def reference(x, conv_w_words, conv_w_scales, gamma, beta):
    x, gamma, beta = f64(x), f64(gamma), f64(beta)
    b, c, h, w = x.shape
    xr = x.reshape(b, c, h * w)
    xq = mxq(xr, 1, "e4m3")
    wt = unpack_weight(conv_w_words, conv_w_scales, FMT)
    y = wt.T @ xq
    mean = y.mean(axis=(0, 2))
    var = (y ** 2).mean(axis=(0, 2)) - mean ** 2
    inv = gamma / np.sqrt(var + EPS)
    y = np.maximum(y * inv[None, :, None] + (beta - mean * inv)[None, :, None], 0.0)
    g = xr @ xr.transpose(0, 2, 1)
    e = np.exp(g - g.max(-1, keepdims=True))
    att = e / e.sum(-1, keepdims=True)
    sp = mxq(att, 2, "e4m3") @ xq
    return (y + sp).reshape(b, c, h, w)

@@ -1,0 +1,196 @@
+from contextlib import ExitStack
+
+import concourse.mybir as mybir
+from concourse.masks import make_identity
+
+F32 = mybir.dt.float32
+BF16 = mybir.dt.bfloat16
+I32 = mybir.dt.int32
+U32 = mybir.dt.uint32
+U8 = mybir.dt.uint8
+FP8X4 = mybir.dt.float8_e4m3fn_x4
+ACT = mybir.ActivationFunctionType
+ALU = mybir.AluOpType
+AXIS = mybir.AxisListType
+
+P = 128
+PACK = 4
+IMAGES = 2
+CHANNELS = 512
+PIXELS = 768
+COLUMNS = IMAGES * PIXELS
+CH_TILES = CHANNELS // P
+PIX_TILES = PIXELS // P
+BANK = 512
+EPS = 1e-5
+
+FLOPS = 3 * 2 * IMAGES * CHANNELS * CHANNELS * PIXELS
+
+
+def tile_informationinteraction_kernel(tc, x, conv_w_words, conv_w_scales, gamma, beta, out):
+    nc = tc.nc
+    x_img = x.rearrange("b c h w -> b c (h w)")
+    out_img = out.rearrange("b c h w -> b c (h w)")
+
+    with ExitStack() as ctx:
+        keep = ctx.enter_context(tc.tile_pool(name="keep", bufs=1))
+        work = ctx.enter_context(tc.tile_pool(name="work", bufs=3))
+        flip_psum = ctx.enter_context(tc.psum_pool(name="flip_psum", bufs=2))
+        gram_psum = ctx.enter_context(tc.psum_pool(name="gram_psum", bufs=3))
+        mx_psum = ctx.enter_context(tc.psum_pool(name="mx_psum", bufs=3))
+
+        x_rows = keep.tile([P, IMAGES, CH_TILES, PIXELS], BF16)
+        x_quads = keep.tile([P, IMAGES, PACK, PIXELS], BF16)
+        nc.sync.dma_start(out=x_rows[:, 0], in_=x_img[0].rearrange("(j p) n -> p j n", p=P))
+        for b in range(IMAGES):
+            nc.sync.dma_start(out=x_quads[:, b], in_=x_img[b].rearrange("(p t) n -> p t n", t=PACK))
+
+        w_codes = keep.tile([P, PACK * CHANNELS], U8, align_bytes=64)
+        nc.sync.dma_start(
+            out=w_codes[:].bitcast(I32),
+            in_=conv_w_words[0].rearrange("p n t -> p (n t)").bitcast(I32),
+        )
+        w_scales = keep.tile([P, CHANNELS], U8, align_bytes=64)
+        nc.vector.memset(w_scales[:].bitcast(I32), 0)
+        for quadrant in range(4):
+            nc.sync.dma_start(
+                out=w_scales[32 * quadrant : 32 * quadrant + 4, :].bitcast(I32),
+                in_=conv_w_scales[0, 4 * quadrant : 4 * quadrant + 4, :].bitcast(I32),
+            )
+        nc.sync.dma_start(out=x_rows[:, 1], in_=x_img[1].rearrange("(j p) n -> p j n", p=P))
+
+        ident = keep.tile([P, P], BF16)
+        make_identity(nc, ident[:])
+
+        affine_rows = keep.tile([P, P], BF16)
+        nc.vector.memset(affine_rows[:], 0.0)
+        nc.scalar.dma_start(out=affine_rows[0:CH_TILES, :], in_=gamma.rearrange("(j p) -> j p", p=P))
+        nc.scalar.dma_start(out=affine_rows[CH_TILES : 2 * CH_TILES, :], in_=beta.rearrange("(j p) -> j p", p=P))
+        affine_ps = flip_psum.tile([P, P], BF16, tag="flip")
+        nc.tensor.transpose(affine_ps[:], affine_rows[:], ident[:])
+        affine = keep.tile([P, 2 * CH_TILES], F32)
+        nc.vector.tensor_copy(out=affine[:], in_=affine_ps[:, 0 : 2 * CH_TILES])
+
+        x_grouped = keep.tile([P, COLUMNS, PACK], BF16, align_bytes=64)
+        x_codes = keep.tile([P, COLUMNS], U32, align_bytes=64)
+        x_scales = keep.tile([P, COLUMNS], U8, align_bytes=64)
+        for b in range(IMAGES):
+            nc.vector.tensor_copy(
+                out=x_grouped[:, b * PIXELS : (b + 1) * PIXELS, :],
+                in_=x_quads[:, b].rearrange("p t n -> p n t"),
+            )
+        for k in range(COLUMNS // BANK):
+            cols = slice(k * BANK, (k + 1) * BANK)
+            nc.vector.quantize_mx(
+                out=x_codes[:, cols].bitcast(FP8X4),
+                scales=x_scales[:, cols],
+                in_=x_grouped[:, cols, :].rearrange("p n t -> p (n t)"),
+            )
+
+        y = keep.tile([P, CH_TILES, COLUMNS], F32)
+        stats = keep.tile([P, CH_TILES, COLUMNS // BANK, 6], F32)
+        for k in range(COLUMNS // BANK):
+            cols = slice(k * BANK, (k + 1) * BANK)
+            for j in range(CH_TILES):
+                y_ps = mx_psum.tile([P, BANK], F32, tag="mx")
+                nc.tensor.matmul_mx(
+                    out=y_ps[:],
+                    lhsT=w_codes[:, PACK * P * j : PACK * P * (j + 1)].bitcast(FP8X4),
+                    lhsT_scale=w_scales[:, P * j : P * (j + 1)],
+                    rhs=x_codes[:, cols].bitcast(FP8X4),
+                    rhs_scale=x_scales[:, cols],
+                    start=True,
+                    stop=True,
+                )
+                nc.scalar.copy(out=y[:, j, cols], in_=y_ps[:])
+                nc.vector.bn_stats(out=stats[:, j, k, :], in_=y[:, j, cols])
+
+        mean_var = keep.tile([P, CH_TILES, 2], F32)
+        for j in range(CH_TILES):
+            nc.vector.bn_aggr(out=mean_var[:, j, :], in_=stats[:, j].rearrange("p k s -> p (k s)"))
+        var_eps = keep.tile([P, CH_TILES], F32)
+        nc.vector.tensor_scalar(out=var_eps[:], in0=mean_var[:, :, 1], scalar1=EPS, scalar2=None, op0=ALU.add)
+        minus_half = keep.tile([P, CH_TILES], F32)
+        nc.gpsimd.memset(minus_half[:], -0.5)
+        rstd = keep.tile([P, CH_TILES], F32)
+        nc.gpsimd.tensor_tensor(out=rstd[:], in0=var_eps[:], in1=minus_half[:], op=ALU.pow)
+        inv = keep.tile([P, CH_TILES], F32)
+        nc.vector.tensor_tensor(out=inv[:], in0=affine[:, 0:CH_TILES], in1=rstd[:], op=ALU.mult)
+        mean_inv = keep.tile([P, CH_TILES], F32)
+        nc.vector.tensor_tensor(out=mean_inv[:], in0=mean_var[:, :, 0], in1=inv[:], op=ALU.mult)
+        shift = keep.tile([P, CH_TILES], F32)
+        nc.vector.tensor_tensor(out=shift[:], in0=affine[:, CH_TILES : 2 * CH_TILES], in1=mean_inv[:], op=ALU.subtract)
+        for j in range(CH_TILES):
+            nc.scalar.activation(
+                out=y[:, j, :], in_=y[:, j, :], func=ACT.Relu, bias=shift[:, j : j + 1], scale=inv[:, j : j + 1]
+            )
+
+        x_flipped = keep.tile([P, IMAGES, PIX_TILES, CHANNELS], BF16)
+        neg_max = keep.tile([P, IMAGES, CH_TILES], F32)
+        row_sum = keep.tile([P, IMAGES, CH_TILES], F32)
+        row_inv = keep.tile([P, IMAGES, CH_TILES], F32)
+        att_codes = keep.tile([P, IMAGES, CHANNELS], U32, align_bytes=64)
+        att_scales = keep.tile([P, IMAGES, CHANNELS], U8, align_bytes=64)
+        for b in range(IMAGES):
+            for i in range(PIX_TILES):
+                x_ps = flip_psum.tile([P, CHANNELS], BF16, tag="flip")
+                for j in range(CH_TILES):
+                    nc.tensor.transpose(x_ps[:, P * j : P * (j + 1)], x_rows[:, b, j, P * i : P * (i + 1)], ident[:])
+                if i % 2 == 0:
+                    nc.scalar.copy(out=x_flipped[:, b, i, :], in_=x_ps[:])
+                else:
+                    nc.vector.tensor_copy(out=x_flipped[:, b, i, :], in_=x_ps[:])
+
+            for j in range(CH_TILES):
+                rows = slice(P * j, P * (j + 1))
+                g_ps = gram_psum.tile([P, CHANNELS], F32, tag="gram")
+                for i in range(PIX_TILES):
+                    nc.tensor.matmul(
+                        out=g_ps[:],
+                        lhsT=x_flipped[:, b, i, rows],
+                        rhs=x_flipped[:, b, i, :],
+                        start=(i == 0),
+                        stop=(i == PIX_TILES - 1),
+                    )
+                nc.vector.tensor_reduce(out=neg_max[:, b, j : j + 1], in_=g_ps[:], axis=AXIS.X, op=ALU.max, negate=True)
+                expo = work.tile([P, PACK, P], F32)
+                nc.scalar.activation(
+                    out=expo[:],
+                    in_=g_ps[:].rearrange("c (p t) -> c t p", t=PACK),
+                    func=ACT.Exp,
+                    bias=neg_max[:, b, j : j + 1],
+                    scale=1.0,
+                    accum_out=row_sum[:, b, j : j + 1],
+                )
+                nc.vector.reciprocal(out=row_inv[:, b, j : j + 1], in_=row_sum[:, b, j : j + 1])
+                att = work.tile([P, PACK, P], BF16)
+                nc.vector.tensor_scalar(
+                    out=att[:], in0=expo[:], scalar1=row_inv[:, b, j : j + 1], scalar2=None, op0=ALU.mult
+                )
+                att_ps = flip_psum.tile([P, PACK, P], BF16, tag="flip")
+                for t in range(PACK):
+                    nc.tensor.transpose(att_ps[:, t, :], att[:, t, :], ident[:])
+                att_grouped = work.tile([P, P, PACK], BF16, align_bytes=64)
+                nc.scalar.copy(out=att_grouped[:], in_=att_ps[:].rearrange("p t c -> p c t"))
+                nc.vector.quantize_mx(
+                    out=att_codes[:, b, rows].bitcast(FP8X4),
+                    scales=att_scales[:, b, rows],
+                    in_=att_grouped[:].rearrange("p c t -> p (c t)"),
+                )
+                result = work.tile([P, PIXELS], F32)
+                for first, width in ((0, BANK), (BANK, PIXELS - BANK)):
+                    cols = slice(b * PIXELS + first, b * PIXELS + first + width)
+                    sp_ps = mx_psum.tile([P, BANK], F32, tag="mx")
+                    nc.tensor.matmul_mx(
+                        out=sp_ps[:, 0:width],
+                        lhsT=att_codes[:, b, rows].bitcast(FP8X4),
+                        lhsT_scale=att_scales[:, b, rows],
+                        rhs=x_codes[:, cols].bitcast(FP8X4),
+                        rhs_scale=x_scales[:, cols],
+                        start=True,
+                        stop=True,
+                    )
+                    nc.vector.tensor_tensor(
+                        out=result[:, first : first + width], in0=sp_ps[:, 0:width], in1=y[:, j, cols], op=ALU.add
+                    )
+                nc.sync.dma_start(out=out_img[b, rows, :], in_=result[:])

@@ -20,8 +20,9 @@ CHANNELS = 512
 PIXELS = 768
 COLUMNS = IMAGES * PIXELS
 CH_TILES = CHANNELS // P
-PIX_TILES = PIXELS // P
+PAIR_TILES = PIXELS // (2 * P)
 BANK = 512
+COL_CHUNKS = COLUMNS // BANK
 EPS = 1e-5
 
 FLOPS = 3 * 2 * IMAGES * CHANNELS * CHANNELS * PIXELS
@@ -34,31 +35,33 @@ def tile_informationinteraction_kernel(tc, x, conv_w_words, conv_w_scales, gamma
 
     with ExitStack() as ctx:
         keep = ctx.enter_context(tc.tile_pool(name="keep", bufs=1))
-        work = ctx.enter_context(tc.tile_pool(name="work", bufs=3))
+        work = ctx.enter_context(tc.tile_pool(name="work", bufs=4))
         flip_psum = ctx.enter_context(tc.psum_pool(name="flip_psum", bufs=2))
         gram_psum = ctx.enter_context(tc.psum_pool(name="gram_psum", bufs=3))
         mx_psum = ctx.enter_context(tc.psum_pool(name="mx_psum", bufs=3))
 
-        x_rows = keep.tile([P, IMAGES, CH_TILES, PIXELS], BF16)
-        x_quads = keep.tile([P, IMAGES, PACK, PIXELS], BF16)
-        nc.sync.dma_start(out=x_rows[:, 0], in_=x_img[0].rearrange("(j p) n -> p j n", p=P))
-        for b in range(IMAGES):
-            nc.sync.dma_start(out=x_quads[:, b], in_=x_img[b].rearrange("(p t) n -> p t n", t=PACK))
-
+        x_quads = [keep.tile([P, PACK, PIXELS], BF16, name="x_quads%d" % b) for b in range(IMAGES)]
         w_codes = keep.tile([P, PACK * CHANNELS], U8, align_bytes=64)
+        w_scales = keep.tile([P, CHANNELS], U8, align_bytes=64)
+        nc.vector.memset(w_scales[:].bitcast(I32), 0)
+
+        def load_quads(b):
+            nc.sync.dma_start(out=x_quads[b][:], in_=x_img[b].rearrange("(p t) n -> p t n", t=PACK))
+
+        load_quads(0)
         nc.sync.dma_start(
             out=w_codes[:].bitcast(I32),
             in_=conv_w_words[0].rearrange("p n t -> p (n t)").bitcast(I32),
         )
-        w_scales = keep.tile([P, CHANNELS], U8, align_bytes=64)
-        nc.vector.memset(w_scales[:].bitcast(I32), 0)
         for quadrant in range(4):
             nc.sync.dma_start(
                 out=w_scales[32 * quadrant : 32 * quadrant + 4, :].bitcast(I32),
                 in_=conv_w_scales[0, 4 * quadrant : 4 * quadrant + 4, :].bitcast(I32),
             )
-        nc.sync.dma_start(out=x_rows[:, 1], in_=x_img[1].rearrange("(j p) n -> p j n", p=P))
+        load_quads(1)
 
+        ident_words = keep.tile([P, P], F32)
+        make_identity(nc, ident_words[:])
         ident = keep.tile([P, P], BF16)
         make_identity(nc, ident[:])
 
@@ -66,20 +69,17 @@ def tile_informationinteraction_kernel(tc, x, conv_w_words, conv_w_scales, gamma
         nc.vector.memset(affine_rows[:], 0.0)
         nc.scalar.dma_start(out=affine_rows[0:CH_TILES, :], in_=gamma.rearrange("(j p) -> j p", p=P))
         nc.scalar.dma_start(out=affine_rows[CH_TILES : 2 * CH_TILES, :], in_=beta.rearrange("(j p) -> j p", p=P))
-        affine_ps = flip_psum.tile([P, P], BF16, tag="flip")
-        nc.tensor.transpose(affine_ps[:], affine_rows[:], ident[:])
-        affine = keep.tile([P, 2 * CH_TILES], F32)
-        nc.vector.tensor_copy(out=affine[:], in_=affine_ps[:, 0 : 2 * CH_TILES])
 
         x_grouped = keep.tile([P, COLUMNS, PACK], BF16, align_bytes=64)
         x_codes = keep.tile([P, COLUMNS], U32, align_bytes=64)
         x_scales = keep.tile([P, COLUMNS], U8, align_bytes=64)
-        for b in range(IMAGES):
-            nc.vector.tensor_copy(
-                out=x_grouped[:, b * PIXELS : (b + 1) * PIXELS, :],
-                in_=x_quads[:, b].rearrange("p t n -> p n t"),
-            )
-        for k in range(COLUMNS // BANK):
+        for b, cut in ((0, BANK), (1, PIXELS - BANK)):
+            for first, last in ((0, cut), (cut, PIXELS)):
+                nc.vector.tensor_copy(
+                    out=x_grouped[:, b * PIXELS + first : b * PIXELS + last, :],
+                    in_=x_quads[b][:, :, first:last].rearrange("p t n -> p n t"),
+                )
+        for k in range(COL_CHUNKS):
             cols = slice(k * BANK, (k + 1) * BANK)
             nc.vector.quantize_mx(
                 out=x_codes[:, cols].bitcast(FP8X4),
@@ -87,9 +87,21 @@ def tile_informationinteraction_kernel(tc, x, conv_w_words, conv_w_scales, gamma
                 in_=x_grouped[:, cols, :].rearrange("p n t -> p (n t)"),
             )
 
+        x_flipped = keep.tile([P, IMAGES, PAIR_TILES, CHANNELS], F32)
+        for b in range(IMAGES):
+            for i in range(PAIR_TILES):
+                pixels = slice(2 * P * i, 2 * P * (i + 1))
+                x_ps = flip_psum.tile([P, PACK, P], F32, tag="flip")
+                for t in range(PACK):
+                    nc.tensor.transpose(x_ps[:, t, :], x_quads[b][:, t, pixels].bitcast(F32), ident_words[:])
+                nc.scalar.copy(
+                    out=x_flipped[:, b, i, :].rearrange("q (p t) -> q p t", t=PACK),
+                    in_=x_ps[:].rearrange("q t p -> q p t"),
+                )
+
         y = keep.tile([P, CH_TILES, COLUMNS], F32)
-        stats = keep.tile([P, CH_TILES, COLUMNS // BANK, 6], F32)
-        for k in range(COLUMNS // BANK):
+        stats = keep.tile([P, CH_TILES, COL_CHUNKS, 6], F32)
+        for k in range(COL_CHUNKS):
             cols = slice(k * BANK, (k + 1) * BANK)
             for j in range(CH_TILES):
                 y_ps = mx_psum.tile([P, BANK], F32, tag="mx")
@@ -104,6 +116,11 @@ def tile_informationinteraction_kernel(tc, x, conv_w_words, conv_w_scales, gamma
                 )
                 nc.scalar.copy(out=y[:, j, cols], in_=y_ps[:])
                 nc.vector.bn_stats(out=stats[:, j, k, :], in_=y[:, j, cols])
+
+        affine_ps = flip_psum.tile([P, P], BF16, tag="flip")
+        nc.tensor.transpose(affine_ps[:], affine_rows[:], ident[:])
+        affine = keep.tile([P, 2 * CH_TILES], F32)
+        nc.vector.tensor_copy(out=affine[:], in_=affine_ps[:, 0 : 2 * CH_TILES])
 
         mean_var = keep.tile([P, CH_TILES, 2], F32)
         for j in range(CH_TILES):
@@ -120,63 +137,68 @@ def tile_informationinteraction_kernel(tc, x, conv_w_words, conv_w_scales, gamma
         nc.vector.tensor_tensor(out=mean_inv[:], in0=mean_var[:, :, 0], in1=inv[:], op=ALU.mult)
         shift = keep.tile([P, CH_TILES], F32)
         nc.vector.tensor_tensor(out=shift[:], in0=affine[:, CH_TILES : 2 * CH_TILES], in1=mean_inv[:], op=ALU.subtract)
-        for j in range(CH_TILES):
-            nc.scalar.activation(
-                out=y[:, j, :], in_=y[:, j, :], func=ACT.Relu, bias=shift[:, j : j + 1], scale=inv[:, j : j + 1]
-            )
+        for b in range(IMAGES):
+            for j in range(CH_TILES):
+                cols = slice(b * PIXELS, (b + 1) * PIXELS)
+                nc.gpsimd.tensor_scalar(
+                    out=y[:, j, cols],
+                    in0=y[:, j, cols],
+                    scalar1=inv[:, j : j + 1],
+                    scalar2=shift[:, j : j + 1],
+                    op0=ALU.mult,
+                    op1=ALU.add,
+                )
 
-        x_flipped = keep.tile([P, IMAGES, PIX_TILES, CHANNELS], BF16)
         neg_max = keep.tile([P, IMAGES, CH_TILES], F32)
         row_sum = keep.tile([P, IMAGES, CH_TILES], F32)
         row_inv = keep.tile([P, IMAGES, CH_TILES], F32)
         att_codes = keep.tile([P, IMAGES, CHANNELS], U32, align_bytes=64)
         att_scales = keep.tile([P, IMAGES, CHANNELS], U8, align_bytes=64)
         for b in range(IMAGES):
-            for i in range(PIX_TILES):
-                x_ps = flip_psum.tile([P, CHANNELS], BF16, tag="flip")
-                for j in range(CH_TILES):
-                    nc.tensor.transpose(x_ps[:, P * j : P * (j + 1)], x_rows[:, b, j, P * i : P * (i + 1)], ident[:])
-                if i % 2 == 0:
-                    nc.scalar.copy(out=x_flipped[:, b, i, :], in_=x_ps[:])
-                else:
-                    nc.vector.tensor_copy(out=x_flipped[:, b, i, :], in_=x_ps[:])
-
             for j in range(CH_TILES):
                 rows = slice(P * j, P * (j + 1))
                 g_ps = gram_psum.tile([P, CHANNELS], F32, tag="gram")
-                for i in range(PIX_TILES):
-                    nc.tensor.matmul(
-                        out=g_ps[:],
-                        lhsT=x_flipped[:, b, i, rows],
-                        rhs=x_flipped[:, b, i, :],
-                        start=(i == 0),
-                        stop=(i == PIX_TILES - 1),
-                    )
+                for i in range(PAIR_TILES):
+                    halves = x_flipped[:, b, i, :].bitcast(BF16).rearrange("q (c e) -> q c e", e=2)
+                    for e in range(2):
+                        nc.tensor.matmul(
+                            out=g_ps[:],
+                            lhsT=halves[:, rows, e],
+                            rhs=halves[:, :, e],
+                            start=(i == 0 and e == 0),
+                            stop=(i == PAIR_TILES - 1 and e == 1),
+                        )
                 nc.vector.tensor_reduce(out=neg_max[:, b, j : j + 1], in_=g_ps[:], axis=AXIS.X, op=ALU.max, negate=True)
-                expo = work.tile([P, PACK, P], F32)
+                expo = work.tile([P, 2, P, 2], F32)
                 nc.scalar.activation(
                     out=expo[:],
-                    in_=g_ps[:].rearrange("c (p t) -> c t p", t=PACK),
+                    in_=g_ps[:].rearrange("c (p u e) -> c u p e", u=2, e=2),
                     func=ACT.Exp,
                     bias=neg_max[:, b, j : j + 1],
                     scale=1.0,
                     accum_out=row_sum[:, b, j : j + 1],
                 )
                 nc.vector.reciprocal(out=row_inv[:, b, j : j + 1], in_=row_sum[:, b, j : j + 1])
-                att = work.tile([P, PACK, P], BF16)
-                nc.vector.tensor_scalar(
-                    out=att[:], in0=expo[:], scalar1=row_inv[:, b, j : j + 1], scalar2=None, op0=ALU.mult
+                att = work.tile([P, 2, 2 * P], BF16)
+                nc.scalar.activation(
+                    out=att[:].rearrange("c u w -> c (u w)"),
+                    in_=expo[:].rearrange("c u p e -> c (u p e)"),
+                    func=ACT.Copy,
+                    scale=row_inv[:, b, j : j + 1],
                 )
-                att_ps = flip_psum.tile([P, PACK, P], BF16, tag="flip")
-                for t in range(PACK):
-                    nc.tensor.transpose(att_ps[:, t, :], att[:, t, :], ident[:])
-                att_grouped = work.tile([P, P, PACK], BF16, align_bytes=64)
-                nc.scalar.copy(out=att_grouped[:], in_=att_ps[:].rearrange("p t c -> p c t"))
+                att_ps = flip_psum.tile([P, 2, P], F32, tag="flip")
+                for u in range(2):
+                    nc.tensor.transpose(att_ps[:, u, :], att[:, u, :].bitcast(F32), ident_words[:])
+                att_grouped = work.tile([P, P, 2], F32, align_bytes=64)
+                nc.scalar.copy(out=att_grouped[:], in_=att_ps[:].rearrange("p u c -> p c u"))
                 nc.vector.quantize_mx(
                     out=att_codes[:, b, rows].bitcast(FP8X4),
                     scales=att_scales[:, b, rows],
-                    in_=att_grouped[:].rearrange("p c t -> p (c t)"),
+                    in_=att_grouped[:].rearrange("p c u -> p (c u)").bitcast(BF16),
                 )
+
+            for j in range(CH_TILES):
+                rows = slice(P * j, P * (j + 1))
                 result = work.tile([P, PIXELS], F32)
                 for first, width in ((0, BANK), (BANK, PIXELS - BANK)):
                     cols = slice(b * PIXELS + first, b * PIXELS + first + width)
@@ -190,7 +212,12 @@ def tile_informationinteraction_kernel(tc, x, conv_w_words, conv_w_scales, gamma
                         start=True,
                         stop=True,
                     )
-                    nc.vector.tensor_tensor(
-                        out=result[:, first : first + width], in0=sp_ps[:, 0:width], in1=y[:, j, cols], op=ALU.add
+                    nc.vector.scalar_tensor_tensor(
+                        out=result[:, first : first + width],
+                        in0=y[:, j, cols],
+                        scalar=0.0,
+                        in1=sp_ps[:, 0:width],
+                        op0=ALU.max,
+                        op1=ALU.add,
                     )
                 nc.sync.dma_start(out=out_img[b, rows, :], in_=result[:])

@@ -60,10 +60,10 @@ def tile_informationinteraction_kernel(tc, x, conv_w_words, conv_w_scales, gamma
             )
         load_quads(1)
 
-        ident_words = keep.tile([P, P], F32)
-        make_identity(nc, ident_words[:])
         ident = keep.tile([P, P], BF16)
         make_identity(nc, ident[:])
+        ident_words = keep.tile([P, P], F32)
+        nc.vector.tensor_copy(out=ident_words[:], in_=ident[:])
 
         affine_rows = keep.tile([P, P], BF16)
         nc.vector.memset(affine_rows[:], 0.0)
@@ -155,6 +155,7 @@ def tile_informationinteraction_kernel(tc, x, conv_w_words, conv_w_scales, gamma
         att_codes = keep.tile([P, IMAGES, CHANNELS], U32, align_bytes=64)
         att_scales = keep.tile([P, IMAGES, CHANNELS], U8, align_bytes=64)
         for b in range(IMAGES):
+            right_of_diagonal = []
             for j in range(CH_TILES):
                 rows = slice(P * j, P * (j + 1))
                 g_ps = gram_psum.tile([P, CHANNELS], F32, tag="gram")
@@ -162,12 +163,22 @@ def tile_informationinteraction_kernel(tc, x, conv_w_words, conv_w_scales, gamma
                     halves = x_flipped[:, b, i, :].bitcast(BF16).rearrange("q (c e) -> q c e", e=2)
                     for e in range(2):
                         nc.tensor.matmul(
-                            out=g_ps[:],
+                            out=g_ps[:, P * j :],
                             lhsT=halves[:, rows, e],
-                            rhs=halves[:, :, e],
+                            rhs=halves[:, P * j :, e],
                             start=(i == 0 and e == 0),
                             stop=(i == PAIR_TILES - 1 and e == 1),
                         )
+                for earlier in range(j):
+                    nc.tensor.transpose(
+                        g_ps[:, P * earlier : P * (earlier + 1)],
+                        right_of_diagonal[earlier][:, P * (j - earlier - 1) : P * (j - earlier)],
+                        ident_words[:],
+                    )
+                if j + 1 < CH_TILES:
+                    kept = work.tile([P, CHANNELS - P * (j + 1)], F32, name="right_of_diagonal%d" % j)
+                    nc.scalar.copy(out=kept[:], in_=g_ps[:, P * (j + 1) :])
+                    right_of_diagonal.append(kept)
                 nc.vector.tensor_reduce(out=neg_max[:, b, j : j + 1], in_=g_ps[:], axis=AXIS.X, op=ALU.max, negate=True)
                 expo = work.tile([P, 2, P, 2], F32)
                 nc.scalar.activation(
@@ -220,4 +231,4 @@ def tile_informationinteraction_kernel(tc, x, conv_w_words, conv_w_scales, gamma
                         op0=ALU.max,
                         op1=ALU.add,
                     )
-                nc.sync.dma_start(out=out_img[b, rows, :], in_=result[:])
+                    nc.sync.dma_start(out=out_img[b, rows, first : first + width], in_=result[:, first : first + width])

@@ -63,7 +63,6 @@ def tile_informationinteraction_kernel(tc, x, conv_w_words, conv_w_scales, gamma
         ident = keep.tile([P, P], BF16)
         make_identity(nc, ident[:])
         ident_words = keep.tile([P, P], F32)
-        nc.vector.tensor_copy(out=ident_words[:], in_=ident[:])
 
         affine_rows = keep.tile([P, P], BF16)
         nc.vector.memset(affine_rows[:], 0.0)
@@ -73,19 +72,28 @@ def tile_informationinteraction_kernel(tc, x, conv_w_words, conv_w_scales, gamma
         x_grouped = keep.tile([P, COLUMNS, PACK], BF16, align_bytes=64)
         x_codes = keep.tile([P, COLUMNS], U32, align_bytes=64)
         x_scales = keep.tile([P, COLUMNS], U8, align_bytes=64)
-        for b, cut in ((0, BANK), (1, PIXELS - BANK)):
+        def regroup(b, cut):
             for first, last in ((0, cut), (cut, PIXELS)):
                 nc.vector.tensor_copy(
                     out=x_grouped[:, b * PIXELS + first : b * PIXELS + last, :],
                     in_=x_quads[b][:, :, first:last].rearrange("p t n -> p n t"),
                 )
-        for k in range(COL_CHUNKS):
+
+        def quantise_x(k):
             cols = slice(k * BANK, (k + 1) * BANK)
             nc.vector.quantize_mx(
                 out=x_codes[:, cols].bitcast(FP8X4),
                 scales=x_scales[:, cols],
                 in_=x_grouped[:, cols, :].rearrange("p n t -> p (n t)"),
             )
+
+        with tc.manual_schedule():
+            nc.vector.tensor_copy(out=ident_words[:], in_=ident[:])
+            regroup(0, BANK)
+            quantise_x(0)
+            regroup(1, PIXELS - BANK)
+            quantise_x(1)
+            quantise_x(2)
 
         x_flipped = keep.tile([P, IMAGES, PAIR_TILES, CHANNELS], F32)
         for b in range(IMAGES):
@@ -126,17 +134,17 @@ def tile_informationinteraction_kernel(tc, x, conv_w_words, conv_w_scales, gamma
         for j in range(CH_TILES):
             nc.vector.bn_aggr(out=mean_var[:, j, :], in_=stats[:, j].rearrange("p k s -> p (k s)"))
         var_eps = keep.tile([P, CH_TILES], F32)
-        nc.vector.tensor_scalar(out=var_eps[:], in0=mean_var[:, :, 1], scalar1=EPS, scalar2=None, op0=ALU.add)
+        nc.gpsimd.tensor_scalar(out=var_eps[:], in0=mean_var[:, :, 1], scalar1=1.0, scalar2=EPS, op0=ALU.mult, op1=ALU.add)
         minus_half = keep.tile([P, CH_TILES], F32)
         nc.gpsimd.memset(minus_half[:], -0.5)
         rstd = keep.tile([P, CH_TILES], F32)
         nc.gpsimd.tensor_tensor(out=rstd[:], in0=var_eps[:], in1=minus_half[:], op=ALU.pow)
         inv = keep.tile([P, CH_TILES], F32)
-        nc.vector.tensor_tensor(out=inv[:], in0=affine[:, 0:CH_TILES], in1=rstd[:], op=ALU.mult)
+        nc.gpsimd.tensor_tensor(out=inv[:], in0=affine[:, 0:CH_TILES], in1=rstd[:], op=ALU.mult)
         mean_inv = keep.tile([P, CH_TILES], F32)
-        nc.vector.tensor_tensor(out=mean_inv[:], in0=mean_var[:, :, 0], in1=inv[:], op=ALU.mult)
+        nc.gpsimd.tensor_tensor(out=mean_inv[:], in0=mean_var[:, :, 0], in1=inv[:], op=ALU.mult)
         shift = keep.tile([P, CH_TILES], F32)
-        nc.vector.tensor_tensor(out=shift[:], in0=affine[:, CH_TILES : 2 * CH_TILES], in1=mean_inv[:], op=ALU.subtract)
+        nc.gpsimd.tensor_tensor(out=shift[:], in0=affine[:, CH_TILES : 2 * CH_TILES], in1=mean_inv[:], op=ALU.subtract)
         for b in range(IMAGES):
             for j in range(CH_TILES):
                 cols = slice(b * PIXELS, (b + 1) * PIXELS)

@@ -23,6 +23,7 @@ CH_TILES = CHANNELS // P
 PAIR_TILES = PIXELS // (2 * P)
 BANK = 512
 COL_CHUNKS = COLUMNS // BANK
+RUN = 4
 EPS = 1e-5
 
 FLOPS = 3 * 2 * IMAGES * CHANNELS * CHANNELS * PIXELS
@@ -75,8 +76,8 @@ def tile_informationinteraction_kernel(tc, x, conv_w_words, conv_w_scales, gamma
         def regroup(b, cut):
             for first, last in ((0, cut), (cut, PIXELS)):
                 nc.vector.tensor_copy(
-                    out=x_grouped[:, b * PIXELS + first : b * PIXELS + last, :],
-                    in_=x_quads[b][:, :, first:last].rearrange("p t n -> p n t"),
+                    out=x_grouped[:, b * PIXELS + first : b * PIXELS + last, :].rearrange("p (n i) t -> p n t i", i=RUN),
+                    in_=x_quads[b][:, :, first:last].rearrange("p t (n i) -> p n t i", i=RUN),
                 )
 
         def quantise_x(k):

@@ -37,6 +37,7 @@ def tile_informationinteraction_kernel(tc, x, conv_w_words, conv_w_scales, gamma
     with ExitStack() as ctx:
         keep = ctx.enter_context(tc.tile_pool(name="keep", bufs=1))
         work = ctx.enter_context(tc.tile_pool(name="work", bufs=4))
+        late = ctx.enter_context(tc.tile_pool(name="late", bufs=2 * IMAGES * CH_TILES))
         flip_psum = ctx.enter_context(tc.psum_pool(name="flip_psum", bufs=2))
         gram_psum = ctx.enter_context(tc.psum_pool(name="gram_psum", bufs=3))
         mx_psum = ctx.enter_context(tc.psum_pool(name="mx_psum", bufs=3))
@@ -73,12 +74,12 @@ def tile_informationinteraction_kernel(tc, x, conv_w_words, conv_w_scales, gamma
         x_grouped = keep.tile([P, COLUMNS, PACK], BF16, align_bytes=64)
         x_codes = keep.tile([P, COLUMNS], U32, align_bytes=64)
         x_scales = keep.tile([P, COLUMNS], U8, align_bytes=64)
-        def regroup(b, cut):
-            for first, last in ((0, cut), (cut, PIXELS)):
-                nc.vector.tensor_copy(
-                    out=x_grouped[:, b * PIXELS + first : b * PIXELS + last, :].rearrange("p (n i) t -> p n t i", i=RUN),
-                    in_=x_quads[b][:, :, first:last].rearrange("p t (n i) -> p n t i", i=RUN),
-                )
+
+        def regroup(b, first, last):
+            nc.vector.tensor_copy(
+                out=x_grouped[:, b * PIXELS + first : b * PIXELS + last, :].rearrange("p (n i) t -> p n t i", i=RUN),
+                in_=x_quads[b][:, :, first:last].rearrange("p t (n i) -> p n t i", i=RUN),
+            )
 
         def quantise_x(k):
             cols = slice(k * BANK, (k + 1) * BANK)
@@ -88,67 +89,154 @@ def tile_informationinteraction_kernel(tc, x, conv_w_words, conv_w_scales, gamma
                 in_=x_grouped[:, cols, :].rearrange("p n t -> p (n t)"),
             )
 
-        with tc.manual_schedule():
-            nc.vector.tensor_copy(out=ident_words[:], in_=ident[:])
-            regroup(0, BANK)
-            quantise_x(0)
-            regroup(1, PIXELS - BANK)
-            quantise_x(1)
-            quantise_x(2)
-
         x_flipped = keep.tile([P, IMAGES, PAIR_TILES, CHANNELS], F32)
-        for b in range(IMAGES):
-            for i in range(PAIR_TILES):
-                pixels = slice(2 * P * i, 2 * P * (i + 1))
-                x_ps = flip_psum.tile([P, PACK, P], F32, tag="flip")
-                for t in range(PACK):
-                    nc.tensor.transpose(x_ps[:, t, :], x_quads[b][:, t, pixels].bitcast(F32), ident_words[:])
-                nc.scalar.copy(
-                    out=x_flipped[:, b, i, :].rearrange("q (p t) -> q p t", t=PACK),
-                    in_=x_ps[:].rearrange("q t p -> q p t"),
-                )
+
+        def flip(b, i):
+            pixels = slice(2 * P * i, 2 * P * (i + 1))
+            x_ps = flip_psum.tile([P, PACK, P], F32, tag="flip")
+            for t in range(PACK):
+                nc.tensor.transpose(x_ps[:, t, :], x_quads[b][:, t, pixels].bitcast(F32), ident_words[:])
+            nc.scalar.copy(
+                out=x_flipped[:, b, i, :].rearrange("q (p t) -> q p t", t=PACK),
+                in_=x_ps[:].rearrange("q t p -> q p t"),
+            )
+
+        stats = keep.tile([P, CH_TILES, COL_CHUNKS, 6], F32)
+
+        def multiply_y(y_ps, j, cols):
+            nc.tensor.matmul_mx(
+                out=y_ps,
+                lhsT=w_codes[:, PACK * P * j : PACK * P * (j + 1)].bitcast(FP8X4),
+                lhsT_scale=w_scales[:, P * j : P * (j + 1)],
+                rhs=x_codes[:, cols].bitcast(FP8X4),
+                rhs_scale=x_scales[:, cols],
+                start=True,
+                stop=True,
+            )
 
         y = keep.tile([P, CH_TILES, COLUMNS], F32)
-        stats = keep.tile([P, CH_TILES, COL_CHUNKS, 6], F32)
-        for k in range(COL_CHUNKS):
+
+        def convolve(k, j):
             cols = slice(k * BANK, (k + 1) * BANK)
-            for j in range(CH_TILES):
-                y_ps = mx_psum.tile([P, BANK], F32, tag="mx")
-                nc.tensor.matmul_mx(
-                    out=y_ps[:],
-                    lhsT=w_codes[:, PACK * P * j : PACK * P * (j + 1)].bitcast(FP8X4),
-                    lhsT_scale=w_scales[:, P * j : P * (j + 1)],
-                    rhs=x_codes[:, cols].bitcast(FP8X4),
-                    rhs_scale=x_scales[:, cols],
-                    start=True,
-                    stop=True,
-                )
-                nc.scalar.copy(out=y[:, j, cols], in_=y_ps[:])
-                nc.vector.bn_stats(out=stats[:, j, k, :], in_=y[:, j, cols])
+            y_ps = mx_psum.tile([P, BANK], F32, tag="mx")
+            multiply_y(y_ps[:], j, cols)
+            nc.scalar.copy(out=y[:, j, cols], in_=y_ps[:])
 
-        affine_ps = flip_psum.tile([P, P], BF16, tag="flip")
-        nc.tensor.transpose(affine_ps[:], affine_rows[:], ident[:])
+        def y_statistics(k, j):
+            nc.vector.bn_stats(out=stats[:, j, k, :], in_=y[:, j, k * BANK : (k + 1) * BANK])
+
         affine = keep.tile([P, 2 * CH_TILES], F32)
-        nc.vector.tensor_copy(out=affine[:], in_=affine_ps[:, 0 : 2 * CH_TILES])
-
         mean_var = keep.tile([P, CH_TILES, 2], F32)
-        for j in range(CH_TILES):
-            nc.vector.bn_aggr(out=mean_var[:, j, :], in_=stats[:, j].rearrange("p k s -> p (k s)"))
         var_eps = keep.tile([P, CH_TILES], F32)
-        nc.gpsimd.tensor_scalar(out=var_eps[:], in0=mean_var[:, :, 1], scalar1=1.0, scalar2=EPS, op0=ALU.mult, op1=ALU.add)
         minus_half = keep.tile([P, CH_TILES], F32)
-        nc.gpsimd.memset(minus_half[:], -0.5)
         rstd = keep.tile([P, CH_TILES], F32)
-        nc.gpsimd.tensor_tensor(out=rstd[:], in0=var_eps[:], in1=minus_half[:], op=ALU.pow)
         inv = keep.tile([P, CH_TILES], F32)
-        nc.gpsimd.tensor_tensor(out=inv[:], in0=affine[:, 0:CH_TILES], in1=rstd[:], op=ALU.mult)
         mean_inv = keep.tile([P, CH_TILES], F32)
-        nc.gpsimd.tensor_tensor(out=mean_inv[:], in0=mean_var[:, :, 0], in1=inv[:], op=ALU.mult)
         shift = keep.tile([P, CH_TILES], F32)
-        nc.gpsimd.tensor_tensor(out=shift[:], in0=affine[:, CH_TILES : 2 * CH_TILES], in1=mean_inv[:], op=ALU.subtract)
-        for b in range(IMAGES):
+        nc.gpsimd.memset(minus_half[:], -0.5)
+
+        def load_affine():
+            affine_ps = flip_psum.tile([P, P], BF16, tag="flip")
+            nc.tensor.transpose(affine_ps[:], affine_rows[:], ident[:])
+            nc.scalar.copy(out=affine[:], in_=affine_ps[:, 0 : 2 * CH_TILES])
+
+        def fold_statistics():
             for j in range(CH_TILES):
-                cols = slice(b * PIXELS, (b + 1) * PIXELS)
+                nc.vector.bn_aggr(out=mean_var[:, j, :], in_=stats[:, j].rearrange("p k s -> p (k s)"))
+            nc.gpsimd.tensor_scalar(out=var_eps[:], in0=mean_var[:, :, 1], scalar1=1.0, scalar2=EPS, op0=ALU.mult, op1=ALU.add)
+            nc.gpsimd.tensor_tensor(out=rstd[:], in0=var_eps[:], in1=minus_half[:], op=ALU.pow)
+            nc.gpsimd.tensor_tensor(out=inv[:], in0=affine[:, 0:CH_TILES], in1=rstd[:], op=ALU.mult)
+            nc.gpsimd.tensor_tensor(out=mean_inv[:], in0=mean_var[:, :, 0], in1=inv[:], op=ALU.mult)
+            nc.gpsimd.tensor_tensor(out=shift[:], in0=affine[:, CH_TILES : 2 * CH_TILES], in1=mean_inv[:], op=ALU.subtract)
+
+        neg_max = keep.tile([P, IMAGES, CH_TILES], F32)
+        row_sum = keep.tile([P, IMAGES, CH_TILES], F32)
+        row_inv = keep.tile([P, IMAGES, CH_TILES], F32)
+        att_codes = keep.tile([P, IMAGES, CHANNELS], U32, align_bytes=64)
+        att_scales = keep.tile([P, IMAGES, CHANNELS], U8, align_bytes=64)
+        gram = {}
+        right_of_diagonal = {}
+        expo = {}
+        att_grouped = {}
+
+        def multiply_gram(b, j):
+            rows = slice(P * j, P * (j + 1))
+            g_ps = gram_psum.tile([P, CHANNELS], F32, tag="gram")
+            gram[b, j] = g_ps
+            for i in range(PAIR_TILES):
+                halves = x_flipped[:, b, i, :].bitcast(BF16).rearrange("q (c e) -> q c e", e=2)
+                for e in range(2):
+                    nc.tensor.matmul(
+                        out=g_ps[:, P * j :],
+                        lhsT=halves[:, rows, e],
+                        rhs=halves[:, P * j :, e],
+                        start=(i == 0 and e == 0),
+                        stop=(i == PAIR_TILES - 1 and e == 1),
+                    )
+            for earlier in range(j):
+                nc.tensor.transpose(
+                    g_ps[:, P * earlier : P * (earlier + 1)],
+                    right_of_diagonal[b, earlier][:, P * (j - earlier - 1) : P * (j - earlier)],
+                    ident_words[:],
+                )
+
+        def keep_right(b, j):
+            if j + 1 < CH_TILES:
+                g_ps = gram[b, j]
+                kept = work.tile([P, CHANNELS - P * (j + 1)], F32, name="right_of_diagonal%d" % j)
+                nc.scalar.copy(out=kept[:], in_=g_ps[:, P * (j + 1) :])
+                right_of_diagonal[b, j] = kept
+
+        def row_maximum(b, j):
+            nc.vector.tensor_reduce(out=neg_max[:, b, j : j + 1], in_=gram[b, j][:], axis=AXIS.X, op=ALU.max, negate=True)
+
+        def softmax(b, j):
+            g_ps = gram[b, j]
+            exponentials = work.tile([P, 2, P, 2], F32, name="exponentials")
+            nc.scalar.activation(
+                out=exponentials[:],
+                in_=g_ps[:].rearrange("c (p u e) -> c u p e", u=2, e=2),
+                func=ACT.Exp,
+                bias=neg_max[:, b, j : j + 1],
+                scale=1.0,
+                accum_out=row_sum[:, b, j : j + 1],
+            )
+            nc.gpsimd.tensor_tensor(out=row_inv[:, b, j : j + 1], in0=row_sum[:, b, j : j + 1], in1=minus_one[:], op=ALU.pow)
+            att = work.tile([P, 2, 2 * P], BF16, name="att")
+            nc.gpsimd.tensor_scalar(
+                out=att[:].rearrange("c u w -> c (u w)"),
+                in0=exponentials[:].rearrange("c u p e -> c (u p e)"),
+                scalar1=row_inv[:, b, j : j + 1],
+                scalar2=0.0,
+                op0=ALU.mult,
+                op1=ALU.add,
+            )
+            expo[b, j] = att
+
+        minus_one = keep.tile([P, 1], F32)
+        nc.gpsimd.memset(minus_one[:], -1.0)
+
+        def turn_att(b, j):
+            att_ps = flip_psum.tile([P, 2, P], F32, tag="flip")
+            for u in range(2):
+                nc.tensor.transpose(att_ps[:, u, :], expo[b, j][:, u, :].bitcast(F32), ident_words[:])
+            grouped = work.tile([P, P, 2], F32, align_bytes=64, name="att_grouped")
+            nc.scalar.copy(out=grouped[:], in_=att_ps[:].rearrange("p u c -> p c u"))
+            att_grouped[b, j] = grouped
+
+        def quantise_att(b, j):
+            rows = slice(P * j, P * (j + 1))
+            nc.vector.quantize_mx(
+                out=att_codes[:, b, rows].bitcast(FP8X4),
+                scales=att_scales[:, b, rows],
+                in_=att_grouped[b, j][:].rearrange("p c u -> p (c u)").bitcast(BF16),
+            )
+
+        def normalise_y(b, j, on_scalar):
+            cols = slice(b * PIXELS, (b + 1) * PIXELS)
+            if on_scalar:
+                nc.scalar.activation(out=y[:, j, cols], in_=y[:, j, cols], func=ACT.Identity, bias=shift[:, j : j + 1], scale=inv[:, j : j + 1])
+            else:
                 nc.gpsimd.tensor_scalar(
                     out=y[:, j, cols],
                     in0=y[:, j, cols],
@@ -158,86 +246,139 @@ def tile_informationinteraction_kernel(tc, x, conv_w_words, conv_w_scales, gamma
                     op1=ALU.add,
                 )
 
-        neg_max = keep.tile([P, IMAGES, CH_TILES], F32)
-        row_sum = keep.tile([P, IMAGES, CH_TILES], F32)
-        row_inv = keep.tile([P, IMAGES, CH_TILES], F32)
-        att_codes = keep.tile([P, IMAGES, CHANNELS], U32, align_bytes=64)
-        att_scales = keep.tile([P, IMAGES, CHANNELS], U8, align_bytes=64)
-        for b in range(IMAGES):
-            right_of_diagonal = []
-            for j in range(CH_TILES):
-                rows = slice(P * j, P * (j + 1))
-                g_ps = gram_psum.tile([P, CHANNELS], F32, tag="gram")
-                for i in range(PAIR_TILES):
-                    halves = x_flipped[:, b, i, :].bitcast(BF16).rearrange("q (c e) -> q c e", e=2)
-                    for e in range(2):
-                        nc.tensor.matmul(
-                            out=g_ps[:, P * j :],
-                            lhsT=halves[:, rows, e],
-                            rhs=halves[:, P * j :, e],
-                            start=(i == 0 and e == 0),
-                            stop=(i == PAIR_TILES - 1 and e == 1),
-                        )
-                for earlier in range(j):
-                    nc.tensor.transpose(
-                        g_ps[:, P * earlier : P * (earlier + 1)],
-                        right_of_diagonal[earlier][:, P * (j - earlier - 1) : P * (j - earlier)],
-                        ident_words[:],
-                    )
-                if j + 1 < CH_TILES:
-                    kept = work.tile([P, CHANNELS - P * (j + 1)], F32, name="right_of_diagonal%d" % j)
-                    nc.scalar.copy(out=kept[:], in_=g_ps[:, P * (j + 1) :])
-                    right_of_diagonal.append(kept)
-                nc.vector.tensor_reduce(out=neg_max[:, b, j : j + 1], in_=g_ps[:], axis=AXIS.X, op=ALU.max, negate=True)
-                expo = work.tile([P, 2, P, 2], F32)
-                nc.scalar.activation(
-                    out=expo[:],
-                    in_=g_ps[:].rearrange("c (p u e) -> c u p e", u=2, e=2),
-                    func=ACT.Exp,
-                    bias=neg_max[:, b, j : j + 1],
-                    scale=1.0,
-                    accum_out=row_sum[:, b, j : j + 1],
-                )
-                nc.vector.reciprocal(out=row_inv[:, b, j : j + 1], in_=row_sum[:, b, j : j + 1])
-                att = work.tile([P, 2, 2 * P], BF16)
-                nc.scalar.activation(
-                    out=att[:].rearrange("c u w -> c (u w)"),
-                    in_=expo[:].rearrange("c u p e -> c (u p e)"),
-                    func=ACT.Copy,
-                    scale=row_inv[:, b, j : j + 1],
-                )
-                att_ps = flip_psum.tile([P, 2, P], F32, tag="flip")
-                for u in range(2):
-                    nc.tensor.transpose(att_ps[:, u, :], att[:, u, :].bitcast(F32), ident_words[:])
-                att_grouped = work.tile([P, P, 2], F32, align_bytes=64)
-                nc.scalar.copy(out=att_grouped[:], in_=att_ps[:].rearrange("p u c -> p c u"))
-                nc.vector.quantize_mx(
-                    out=att_codes[:, b, rows].bitcast(FP8X4),
-                    scales=att_scales[:, b, rows],
-                    in_=att_grouped[:].rearrange("p c u -> p (c u)").bitcast(BF16),
-                )
+        def emit(b, j, first, width):
+            rows = slice(P * j, P * (j + 1))
+            cols = slice(b * PIXELS + first, b * PIXELS + first + width)
+            sp_ps = mx_psum.tile([P, BANK], F32, tag="mx")
+            nc.tensor.matmul_mx(
+                out=sp_ps[:, 0:width],
+                lhsT=att_codes[:, b, rows].bitcast(FP8X4),
+                lhsT_scale=att_scales[:, b, rows],
+                rhs=x_codes[:, cols].bitcast(FP8X4),
+                rhs_scale=x_scales[:, cols],
+                start=True,
+                stop=True,
+            )
+            result = late.tile([P, BANK], F32, name="result")
+            nc.vector.scalar_tensor_tensor(
+                out=result[:, 0:width],
+                in0=y[:, j, cols],
+                scalar=0.0,
+                in1=sp_ps[:, 0:width],
+                op0=ALU.max,
+                op1=ALU.add,
+            )
+            nc.sync.dma_start(out=out_img[b, rows, first : first + width], in_=result[:, 0:width])
 
-            for j in range(CH_TILES):
-                rows = slice(P * j, P * (j + 1))
-                result = work.tile([P, PIXELS], F32)
-                for first, width in ((0, BANK), (BANK, PIXELS - BANK)):
-                    cols = slice(b * PIXELS + first, b * PIXELS + first + width)
-                    sp_ps = mx_psum.tile([P, BANK], F32, tag="mx")
-                    nc.tensor.matmul_mx(
-                        out=sp_ps[:, 0:width],
-                        lhsT=att_codes[:, b, rows].bitcast(FP8X4),
-                        lhsT_scale=att_scales[:, b, rows],
-                        rhs=x_codes[:, cols].bitcast(FP8X4),
-                        rhs_scale=x_scales[:, cols],
-                        start=True,
-                        stop=True,
-                    )
-                    nc.vector.scalar_tensor_tensor(
-                        out=result[:, first : first + width],
-                        in0=y[:, j, cols],
-                        scalar=0.0,
-                        in1=sp_ps[:, 0:width],
-                        op0=ALU.max,
-                        op1=ALU.add,
-                    )
-                    nc.sync.dma_start(out=out_img[b, rows, first : first + width], in_=result[:, first : first + width])
+        pieces = [(0, BANK), (BANK, PIXELS - BANK)]
+        with tc.manual_schedule():
+            nc.vector.tensor_copy(out=ident_words[:], in_=ident[:])
+            regroup(0, 0, BANK)
+            quantise_x(0)
+            regroup(0, BANK, PIXELS)
+            flip(0, 0)
+            flip(0, 1)
+            flip(0, 2)
+            convolve(0, 0)
+            convolve(0, 1)
+            convolve(0, 2)
+            convolve(0, 3)
+            multiply_gram(0, 0)
+            keep_right(0, 0)
+            regroup(1, 0, PIXELS - BANK)
+            quantise_x(1)
+            regroup(1, PIXELS - BANK, PIXELS)
+            quantise_x(2)
+            flip(1, 0)
+            flip(1, 1)
+            flip(1, 2)
+            row_maximum(0, 0)
+            softmax(0, 0)
+            y_statistics(0, 0)
+            y_statistics(0, 1)
+            multiply_gram(0, 1)
+            keep_right(0, 1)
+            convolve(1, 0)
+            convolve(1, 1)
+            row_maximum(0, 1)
+            softmax(0, 1)
+            y_statistics(0, 2)
+            y_statistics(0, 3)
+            load_affine()
+            turn_att(0, 0)
+            multiply_gram(0, 2)
+            keep_right(0, 2)
+            convolve(1, 2)
+            convolve(1, 3)
+            row_maximum(0, 2)
+            softmax(0, 2)
+            y_statistics(1, 0)
+            y_statistics(1, 1)
+            quantise_att(0, 0)
+            turn_att(0, 1)
+            multiply_gram(0, 3)
+            row_maximum(0, 3)
+            softmax(0, 3)
+            convolve(2, 0)
+            convolve(2, 1)
+            y_statistics(1, 2)
+            y_statistics(1, 3)
+            quantise_att(0, 1)
+            turn_att(0, 2)
+            multiply_gram(1, 0)
+            keep_right(1, 0)
+            convolve(2, 2)
+            convolve(2, 3)
+            y_statistics(2, 0)
+            y_statistics(2, 1)
+            quantise_att(0, 2)
+            turn_att(0, 3)
+            multiply_gram(1, 1)
+            keep_right(1, 1)
+            row_maximum(1, 0)
+            y_statistics(2, 2)
+            quantise_att(0, 3)
+            y_statistics(2, 3)
+            fold_statistics()
+            softmax(1, 0)
+            row_maximum(1, 1)
+            softmax(1, 1)
+            multiply_gram(1, 2)
+            keep_right(1, 2)
+            turn_att(1, 0)
+            normalise_y(0, 0, True)
+            normalise_y(0, 1, False)
+            emit(0, 0, 0, BANK)
+            emit(0, 0, BANK, PIXELS - BANK)
+            row_maximum(1, 2)
+            softmax(1, 2)
+            quantise_att(1, 0)
+            turn_att(1, 1)
+            multiply_gram(1, 3)
+            emit(0, 1, 0, BANK)
+            emit(0, 1, BANK, PIXELS - BANK)
+            normalise_y(0, 2, True)
+            normalise_y(0, 3, False)
+            row_maximum(1, 3)
+            softmax(1, 3)
+            quantise_att(1, 1)
+            turn_att(1, 2)
+            emit(0, 2, 0, BANK)
+            emit(0, 2, BANK, PIXELS - BANK)
+            quantise_att(1, 2)
+            turn_att(1, 3)
+            emit(0, 3, 0, BANK)
+            emit(0, 3, BANK, PIXELS - BANK)
+            normalise_y(1, 0, True)
+            normalise_y(1, 1, False)
+            quantise_att(1, 3)
+            emit(1, 0, 0, BANK)
+            emit(1, 0, BANK, PIXELS - BANK)
+            normalise_y(1, 2, True)
+            normalise_y(1, 3, False)
+            emit(1, 1, 0, BANK)
+            emit(1, 1, BANK, PIXELS - BANK)
+            emit(1, 2, 0, BANK)
+            emit(1, 2, BANK, PIXELS - BANK)
+            emit(1, 3, 0, BANK)
+            emit(1, 3, BANK, PIXELS - BANK)

@@ -47,10 +47,14 @@ def tile_informationinteraction_kernel(tc, x, conv_w_words, conv_w_scales, gamma
         w_scales = keep.tile([P, CHANNELS], U8, align_bytes=64)
         nc.vector.memset(w_scales[:].bitcast(I32), 0)
 
-        def load_quads(b):
-            nc.sync.dma_start(out=x_quads[b][:], in_=x_img[b].rearrange("(p t) n -> p t n", t=PACK))
+        def load_quads(b, first, last):
+            nc.sync.dma_start(
+                out=x_quads[b][:, :, first:last], in_=x_img[b].rearrange("(p t) n -> p t n", t=PACK)[:, :, first:last]
+            )
 
-        load_quads(0)
+        load_quads(0, 0, BANK)
+        load_quads(0, BANK, PIXELS)
+        load_quads(1, 0, PIXELS)
         nc.sync.dma_start(
             out=w_codes[:].bitcast(I32),
             in_=conv_w_words[0].rearrange("p n t -> p (n t)").bitcast(I32),
@@ -60,7 +64,6 @@ def tile_informationinteraction_kernel(tc, x, conv_w_words, conv_w_scales, gamma
                 out=w_scales[32 * quadrant : 32 * quadrant + 4, :].bitcast(I32),
                 in_=conv_w_scales[0, 4 * quadrant : 4 * quadrant + 4, :].bitcast(I32),
             )
-        load_quads(1)
 
         ident = keep.tile([P, P], BF16)
         make_identity(nc, ident[:])
@@ -75,8 +78,8 @@ def tile_informationinteraction_kernel(tc, x, conv_w_words, conv_w_scales, gamma
         x_codes = keep.tile([P, COLUMNS], U32, align_bytes=64)
         x_scales = keep.tile([P, COLUMNS], U8, align_bytes=64)
 
-        def regroup(b, first, last):
-            nc.vector.tensor_copy(
+        def regroup(b, first, last, copy=nc.vector.tensor_copy):
+            copy(
                 out=x_grouped[:, b * PIXELS + first : b * PIXELS + last, :].rearrange("p (n i) t -> p n t i", i=RUN),
                 in_=x_quads[b][:, :, first:last].rearrange("p t (n i) -> p n t i", i=RUN),
             )
@@ -91,14 +94,19 @@ def tile_informationinteraction_kernel(tc, x, conv_w_words, conv_w_scales, gamma
 
         x_flipped = keep.tile([P, IMAGES, PAIR_TILES, CHANNELS], F32)
 
-        def flip(b, i):
+        flipped = {}
+
+        def turn_x(b, i):
             pixels = slice(2 * P * i, 2 * P * (i + 1))
             x_ps = flip_psum.tile([P, PACK, P], F32, tag="flip")
             for t in range(PACK):
                 nc.tensor.transpose(x_ps[:, t, :], x_quads[b][:, t, pixels].bitcast(F32), ident_words[:])
+            flipped[b, i] = x_ps
+
+        def keep_flipped(b, i):
             nc.scalar.copy(
                 out=x_flipped[:, b, i, :].rearrange("q (p t) -> q p t", t=PACK),
-                in_=x_ps[:].rearrange("q t p -> q p t"),
+                in_=flipped[b, i][:].rearrange("q t p -> q p t"),
             )
 
         stats = keep.tile([P, CH_TILES, COL_CHUNKS, 6], F32)
@@ -114,16 +122,15 @@ def tile_informationinteraction_kernel(tc, x, conv_w_words, conv_w_scales, gamma
                 stop=True,
             )
 
-        y = keep.tile([P, CH_TILES, COLUMNS], F32)
+        y_psum = {}
 
         def convolve(k, j):
-            cols = slice(k * BANK, (k + 1) * BANK)
             y_ps = mx_psum.tile([P, BANK], F32, tag="mx")
-            multiply_y(y_ps[:], j, cols)
-            nc.scalar.copy(out=y[:, j, cols], in_=y_ps[:])
+            multiply_y(y_ps[:], j, slice(k * BANK, (k + 1) * BANK))
+            y_psum[k, j] = y_ps
 
         def y_statistics(k, j):
-            nc.vector.bn_stats(out=stats[:, j, k, :], in_=y[:, j, k * BANK : (k + 1) * BANK])
+            nc.vector.bn_stats(out=stats[:, j, k, :], in_=y_psum[k, j][:])
 
         affine = keep.tile([P, 2 * CH_TILES], F32)
         mean_var = keep.tile([P, CH_TILES, 2], F32)
@@ -140,11 +147,13 @@ def tile_informationinteraction_kernel(tc, x, conv_w_words, conv_w_scales, gamma
             nc.tensor.transpose(affine_ps[:], affine_rows[:], ident[:])
             nc.scalar.copy(out=affine[:], in_=affine_ps[:, 0 : 2 * CH_TILES])
 
-        def fold_statistics():
+        def aggregate_statistics():
             for j in range(CH_TILES):
                 nc.vector.bn_aggr(out=mean_var[:, j, :], in_=stats[:, j].rearrange("p k s -> p (k s)"))
             nc.gpsimd.tensor_scalar(out=var_eps[:], in0=mean_var[:, :, 1], scalar1=1.0, scalar2=EPS, op0=ALU.mult, op1=ALU.add)
             nc.gpsimd.tensor_tensor(out=rstd[:], in0=var_eps[:], in1=minus_half[:], op=ALU.pow)
+
+        def fold_statistics():
             nc.gpsimd.tensor_tensor(out=inv[:], in0=affine[:, 0:CH_TILES], in1=rstd[:], op=ALU.mult)
             nc.gpsimd.tensor_tensor(out=mean_inv[:], in0=mean_var[:, :, 0], in1=inv[:], op=ALU.mult)
             nc.gpsimd.tensor_tensor(out=shift[:], in0=affine[:, CH_TILES : 2 * CH_TILES], in1=mean_inv[:], op=ALU.subtract)
@@ -157,6 +166,8 @@ def tile_informationinteraction_kernel(tc, x, conv_w_words, conv_w_scales, gamma
         gram = {}
         right_of_diagonal = {}
         expo = {}
+        att = {}
+        att_psum = {}
         att_grouped = {}
 
         def multiply_gram(b, j):
@@ -201,27 +212,32 @@ def tile_informationinteraction_kernel(tc, x, conv_w_words, conv_w_scales, gamma
                 scale=1.0,
                 accum_out=row_sum[:, b, j : j + 1],
             )
-            nc.gpsimd.tensor_tensor(out=row_inv[:, b, j : j + 1], in0=row_sum[:, b, j : j + 1], in1=minus_one[:], op=ALU.pow)
-            att = work.tile([P, 2, 2 * P], BF16, name="att")
+            expo[b, j] = exponentials
+
+        def invert_sum(b, j):
+            nc.vector.reciprocal(out=row_inv[:, b, j : j + 1], in_=row_sum[:, b, j : j + 1])
+
+        def divide(b, j):
+            divided = work.tile([P, 2, 2 * P], BF16, name="divided")
             nc.gpsimd.tensor_scalar(
-                out=att[:].rearrange("c u w -> c (u w)"),
-                in0=exponentials[:].rearrange("c u p e -> c (u p e)"),
+                out=divided[:].rearrange("c u w -> c (u w)"),
+                in0=expo[b, j][:].rearrange("c u p e -> c (u p e)"),
                 scalar1=row_inv[:, b, j : j + 1],
                 scalar2=0.0,
                 op0=ALU.mult,
                 op1=ALU.add,
             )
-            expo[b, j] = att
-
-        minus_one = keep.tile([P, 1], F32)
-        nc.gpsimd.memset(minus_one[:], -1.0)
+            att[b, j] = divided
 
         def turn_att(b, j):
             att_ps = flip_psum.tile([P, 2, P], F32, tag="flip")
             for u in range(2):
-                nc.tensor.transpose(att_ps[:, u, :], expo[b, j][:, u, :].bitcast(F32), ident_words[:])
+                nc.tensor.transpose(att_ps[:, u, :], att[b, j][:, u, :].bitcast(F32), ident_words[:])
+            att_psum[b, j] = att_ps
+
+        def group_att(b, j):
             grouped = work.tile([P, P, 2], F32, align_bytes=64, name="att_grouped")
-            nc.scalar.copy(out=grouped[:], in_=att_ps[:].rearrange("p u c -> p c u"))
+            nc.scalar.copy(out=grouped[:], in_=att_psum[b, j][:].rearrange("p u c -> p c u"))
             att_grouped[b, j] = grouped
 
         def quantise_att(b, j):
@@ -232,24 +248,32 @@ def tile_informationinteraction_kernel(tc, x, conv_w_words, conv_w_scales, gamma
                 in_=att_grouped[b, j][:].rearrange("p c u -> p (c u)").bitcast(BF16),
             )
 
-        def normalise_y(b, j, on_scalar):
-            cols = slice(b * PIXELS, (b + 1) * PIXELS)
-            if on_scalar:
-                nc.scalar.activation(out=y[:, j, cols], in_=y[:, j, cols], func=ACT.Identity, bias=shift[:, j : j + 1], scale=inv[:, j : j + 1])
-            else:
-                nc.gpsimd.tensor_scalar(
-                    out=y[:, j, cols],
-                    in0=y[:, j, cols],
-                    scalar1=inv[:, j : j + 1],
-                    scalar2=shift[:, j : j + 1],
-                    op0=ALU.mult,
-                    op1=ALU.add,
-                )
+        y_act = {}
 
-        def emit(b, j, first, width):
+        y_psum2 = {}
+
+        def repeat_y(b, j, first, width):
+            y_ps = mx_psum.tile([P, BANK], F32, tag="mx")
+            multiply_y(y_ps[:, 0:width], j, slice(b * PIXELS + first, b * PIXELS + first + width))
+            y_psum2[b, j, first] = y_ps
+
+        def activate_y(b, j, first, width):
+            activated = late.tile([P, BANK], F32, name="activated")
+            nc.scalar.activation(
+                out=activated[:, 0:width],
+                in_=y_psum2[b, j, first][:, 0:width],
+                func=ACT.Relu,
+                bias=shift[:, j : j + 1],
+                scale=inv[:, j : j + 1],
+            )
+            y_act[b, j, first] = activated
+
+        sp_psum = {}
+
+        def multiply_sp(b, j, first, width):
             rows = slice(P * j, P * (j + 1))
             cols = slice(b * PIXELS + first, b * PIXELS + first + width)
-            sp_ps = mx_psum.tile([P, BANK], F32, tag="mx")
+            sp_ps = gram_psum.tile([P, BANK], F32, tag="gram")
             nc.tensor.matmul_mx(
                 out=sp_ps[:, 0:width],
                 lhsT=att_codes[:, b, rows].bitcast(FP8X4),
@@ -259,126 +283,195 @@ def tile_informationinteraction_kernel(tc, x, conv_w_words, conv_w_scales, gamma
                 start=True,
                 stop=True,
             )
+            sp_psum[b, j, first] = sp_ps
+
+        def emit(b, j, first, width):
+            rows = slice(P * j, P * (j + 1))
             result = late.tile([P, BANK], F32, name="result")
-            nc.vector.scalar_tensor_tensor(
-                out=result[:, 0:width],
-                in0=y[:, j, cols],
-                scalar=0.0,
-                in1=sp_ps[:, 0:width],
-                op0=ALU.max,
-                op1=ALU.add,
-            )
+            nc.vector.tensor_tensor(out=result[:, 0:width], in0=y_act[b, j, first][:, 0:width], in1=sp_psum[b, j, first][:, 0:width], op=ALU.add)
             nc.sync.dma_start(out=out_img[b, rows, first : first + width], in_=result[:, 0:width])
 
         pieces = [(0, BANK), (BANK, PIXELS - BANK)]
         with tc.manual_schedule():
             nc.vector.tensor_copy(out=ident_words[:], in_=ident[:])
             regroup(0, 0, BANK)
-            quantise_x(0)
             regroup(0, BANK, PIXELS)
-            flip(0, 0)
-            flip(0, 1)
-            flip(0, 2)
+            quantise_x(0)
+            turn_x(0, 0)
+            keep_flipped(0, 0)
+            turn_x(0, 1)
+            keep_flipped(0, 1)
+            turn_x(0, 2)
+            keep_flipped(0, 2)
+            regroup(1, BANK, PIXELS, nc.scalar.copy)
+            regroup(1, 0, PIXELS - BANK)
+            regroup(1, PIXELS - BANK, BANK)
+            quantise_x(1)
+            multiply_gram(0, 0)
+            keep_right(0, 0)
             convolve(0, 0)
             convolve(0, 1)
             convolve(0, 2)
-            convolve(0, 3)
-            multiply_gram(0, 0)
-            keep_right(0, 0)
-            regroup(1, 0, PIXELS - BANK)
-            quantise_x(1)
-            regroup(1, PIXELS - BANK, PIXELS)
-            quantise_x(2)
-            flip(1, 0)
-            flip(1, 1)
-            flip(1, 2)
+            y_statistics(0, 0)
             row_maximum(0, 0)
             softmax(0, 0)
-            y_statistics(0, 0)
+            quantise_x(2)
             y_statistics(0, 1)
+            y_statistics(0, 2)
             multiply_gram(0, 1)
             keep_right(0, 1)
+            convolve(0, 3)
+            turn_x(1, 0)
+            keep_flipped(1, 0)
             convolve(1, 0)
             convolve(1, 1)
             row_maximum(0, 1)
             softmax(0, 1)
-            y_statistics(0, 2)
+            invert_sum(0, 0)
+            divide(0, 0)
             y_statistics(0, 3)
-            load_affine()
-            turn_att(0, 0)
+            y_statistics(1, 0)
+            y_statistics(1, 1)
             multiply_gram(0, 2)
             keep_right(0, 2)
+            turn_x(1, 1)
+            keep_flipped(1, 1)
             convolve(1, 2)
             convolve(1, 3)
             row_maximum(0, 2)
             softmax(0, 2)
-            y_statistics(1, 0)
-            y_statistics(1, 1)
-            quantise_att(0, 0)
-            turn_att(0, 1)
-            multiply_gram(0, 3)
-            row_maximum(0, 3)
-            softmax(0, 3)
-            convolve(2, 0)
-            convolve(2, 1)
+            invert_sum(0, 1)
+            divide(0, 1)
+            load_affine()
             y_statistics(1, 2)
             y_statistics(1, 3)
-            quantise_att(0, 1)
-            turn_att(0, 2)
+            multiply_gram(0, 3)
+            turn_x(1, 2)
+            keep_flipped(1, 2)
+            convolve(2, 0)
+            convolve(2, 1)
+            row_maximum(0, 3)
+            softmax(0, 3)
+            invert_sum(0, 2)
+            divide(0, 2)
+            y_statistics(2, 0)
+            y_statistics(2, 1)
             multiply_gram(1, 0)
             keep_right(1, 0)
             convolve(2, 2)
             convolve(2, 3)
-            y_statistics(2, 0)
-            y_statistics(2, 1)
-            quantise_att(0, 2)
-            turn_att(0, 3)
+            turn_att(0, 0)
+            group_att(0, 0)
+            y_statistics(2, 2)
+            row_maximum(1, 0)
+            softmax(1, 0)
+            invert_sum(0, 3)
+            divide(0, 3)
+            y_statistics(2, 3)
+            aggregate_statistics()
+            fold_statistics()
             multiply_gram(1, 1)
             keep_right(1, 1)
-            row_maximum(1, 0)
-            y_statistics(2, 2)
-            quantise_att(0, 3)
-            y_statistics(2, 3)
-            fold_statistics()
-            softmax(1, 0)
+            turn_att(0, 1)
+            group_att(0, 1)
             row_maximum(1, 1)
             softmax(1, 1)
+            invert_sum(1, 0)
+            divide(1, 0)
+            quantise_att(0, 0)
+            quantise_att(0, 1)
             multiply_gram(1, 2)
             keep_right(1, 2)
-            turn_att(1, 0)
-            normalise_y(0, 0, True)
-            normalise_y(0, 1, False)
-            emit(0, 0, 0, BANK)
-            emit(0, 0, BANK, PIXELS - BANK)
+            turn_att(0, 2)
+            group_att(0, 2)
             row_maximum(1, 2)
             softmax(1, 2)
-            quantise_att(1, 0)
-            turn_att(1, 1)
+            invert_sum(1, 1)
+            divide(1, 1)
+            quantise_att(0, 2)
+            repeat_y(0, 0, 0, BANK)
+            repeat_y(0, 0, BANK, PIXELS - BANK)
             multiply_gram(1, 3)
-            emit(0, 1, 0, BANK)
-            emit(0, 1, BANK, PIXELS - BANK)
-            normalise_y(0, 2, True)
-            normalise_y(0, 3, False)
+            turn_att(0, 3)
+            group_att(0, 3)
+            activate_y(0, 0, 0, BANK)
+            activate_y(0, 0, BANK, PIXELS - BANK)
             row_maximum(1, 3)
             softmax(1, 3)
-            quantise_att(1, 1)
-            turn_att(1, 2)
+            invert_sum(1, 2)
+            divide(1, 2)
+            quantise_att(0, 3)
+            multiply_sp(0, 0, 0, BANK)
+            multiply_sp(0, 0, BANK, PIXELS - BANK)
+            repeat_y(0, 1, 0, BANK)
+            repeat_y(0, 1, BANK, PIXELS - BANK)
+            emit(0, 0, 0, BANK)
+            turn_att(1, 0)
+            group_att(1, 0)
+            activate_y(0, 1, 0, BANK)
+            emit(0, 0, BANK, PIXELS - BANK)
+            activate_y(0, 1, BANK, PIXELS - BANK)
+            multiply_sp(0, 1, 0, BANK)
+            multiply_sp(0, 1, BANK, PIXELS - BANK)
+            invert_sum(1, 3)
+            divide(1, 3)
+            repeat_y(0, 2, 0, BANK)
+            repeat_y(0, 2, BANK, PIXELS - BANK)
+            emit(0, 1, 0, BANK)
+            activate_y(0, 2, 0, BANK)
+            emit(0, 1, BANK, PIXELS - BANK)
+            turn_att(1, 1)
+            group_att(1, 1)
+            quantise_att(1, 0)
+            activate_y(0, 2, BANK, PIXELS - BANK)
+            multiply_sp(0, 2, 0, BANK)
+            multiply_sp(0, 2, BANK, PIXELS - BANK)
+            repeat_y(0, 3, 0, BANK)
+            repeat_y(0, 3, BANK, PIXELS - BANK)
             emit(0, 2, 0, BANK)
+            activate_y(0, 3, 0, BANK)
             emit(0, 2, BANK, PIXELS - BANK)
-            quantise_att(1, 2)
-            turn_att(1, 3)
+            turn_att(1, 2)
+            group_att(1, 2)
+            quantise_att(1, 1)
+            activate_y(0, 3, BANK, PIXELS - BANK)
+            multiply_sp(0, 3, 0, BANK)
+            multiply_sp(0, 3, BANK, PIXELS - BANK)
+            repeat_y(1, 0, 0, BANK)
+            repeat_y(1, 0, BANK, PIXELS - BANK)
             emit(0, 3, 0, BANK)
+            activate_y(1, 0, 0, BANK)
             emit(0, 3, BANK, PIXELS - BANK)
-            normalise_y(1, 0, True)
-            normalise_y(1, 1, False)
-            quantise_att(1, 3)
+            turn_att(1, 3)
+            group_att(1, 3)
+            quantise_att(1, 2)
+            activate_y(1, 0, BANK, PIXELS - BANK)
+            multiply_sp(1, 0, 0, BANK)
+            multiply_sp(1, 0, BANK, PIXELS - BANK)
+            repeat_y(1, 1, 0, BANK)
+            repeat_y(1, 1, BANK, PIXELS - BANK)
             emit(1, 0, 0, BANK)
+            activate_y(1, 1, 0, BANK)
             emit(1, 0, BANK, PIXELS - BANK)
-            normalise_y(1, 2, True)
-            normalise_y(1, 3, False)
+            quantise_att(1, 3)
+            activate_y(1, 1, BANK, PIXELS - BANK)
+            multiply_sp(1, 1, 0, BANK)
+            multiply_sp(1, 1, BANK, PIXELS - BANK)
+            repeat_y(1, 2, 0, BANK)
+            repeat_y(1, 2, BANK, PIXELS - BANK)
             emit(1, 1, 0, BANK)
+            activate_y(1, 2, 0, BANK)
             emit(1, 1, BANK, PIXELS - BANK)
+            activate_y(1, 2, BANK, PIXELS - BANK)
+            multiply_sp(1, 2, 0, BANK)
+            multiply_sp(1, 2, BANK, PIXELS - BANK)
+            repeat_y(1, 3, 0, BANK)
+            repeat_y(1, 3, BANK, PIXELS - BANK)
             emit(1, 2, 0, BANK)
+            activate_y(1, 3, 0, BANK)
             emit(1, 2, BANK, PIXELS - BANK)
+            activate_y(1, 3, BANK, PIXELS - BANK)
+            multiply_sp(1, 3, 0, BANK)
+            multiply_sp(1, 3, BANK, PIXELS - BANK)
             emit(1, 3, 0, BANK)
             emit(1, 3, BANK, PIXELS - BANK)

@@ -94,11 +94,22 @@ def tile_informationinteraction_kernel(tc, x, conv_w_words, conv_w_scales, gamma
 
         x_flipped = keep.tile([P, IMAGES, PAIR_TILES, CHANNELS], F32)
 
+        idle = keep.tile([P, BANK], BF16)
+        nc.vector.memset(idle[:], 0.0)
+
+        def warm_up(n):
+            idle_ps = mx_psum.tile([P, BANK], F32, tag="mx")
+            for i in range(n):
+                nc.tensor.matmul(out=idle_ps[:], lhsT=idle[:, 0:P], rhs=idle[:], start=True, stop=True)
+
         flipped = {}
 
         def turn_x(b, i):
             pixels = slice(2 * P * i, 2 * P * (i + 1))
-            x_ps = flip_psum.tile([P, PACK, P], F32, tag="flip")
+            if b == 0 and i == 2:
+                x_ps = mx_psum.tile([P, PACK, P], F32, tag="mx")
+            else:
+                x_ps = flip_psum.tile([P, PACK, P], F32, tag="flip")
             for t in range(PACK):
                 nc.tensor.transpose(x_ps[:, t, :], x_quads[b][:, t, pixels].bitcast(F32), ident_words[:])
             flipped[b, i] = x_ps
@@ -294,6 +305,7 @@ def tile_informationinteraction_kernel(tc, x, conv_w_words, conv_w_scales, gamma
         pieces = [(0, BANK), (BANK, PIXELS - BANK)]
         with tc.manual_schedule():
             nc.vector.tensor_copy(out=ident_words[:], in_=ident[:])
+            warm_up(5)
             regroup(0, 0, BANK)
             regroup(0, BANK, PIXELS)
             quantise_x(0)
@@ -310,8 +322,10 @@ def tile_informationinteraction_kernel(tc, x, conv_w_words, conv_w_scales, gamma
             multiply_gram(0, 0)
             keep_right(0, 0)
             convolve(0, 0)
+            turn_x(1, 0)
             convolve(0, 1)
             convolve(0, 2)
+            keep_flipped(1, 0)
             y_statistics(0, 0)
             row_maximum(0, 0)
             softmax(0, 0)
@@ -321,9 +335,9 @@ def tile_informationinteraction_kernel(tc, x, conv_w_words, conv_w_scales, gamma
             multiply_gram(0, 1)
             keep_right(0, 1)
             convolve(0, 3)
-            turn_x(1, 0)
-            keep_flipped(1, 0)
             convolve(1, 0)
+            turn_x(1, 1)
+            keep_flipped(1, 1)
             convolve(1, 1)
             row_maximum(0, 1)
             softmax(0, 1)
@@ -334,8 +348,8 @@ def tile_informationinteraction_kernel(tc, x, conv_w_words, conv_w_scales, gamma
             y_statistics(1, 1)
             multiply_gram(0, 2)
             keep_right(0, 2)
-            turn_x(1, 1)
-            keep_flipped(1, 1)
+            turn_x(1, 2)
+            keep_flipped(1, 2)
             convolve(1, 2)
             convolve(1, 3)
             row_maximum(0, 2)
@@ -346,8 +360,6 @@ def tile_informationinteraction_kernel(tc, x, conv_w_words, conv_w_scales, gamma
             y_statistics(1, 2)
             y_statistics(1, 3)
             multiply_gram(0, 3)
-            turn_x(1, 2)
-            keep_flipped(1, 2)
             convolve(2, 0)
             convolve(2, 1)
             row_maximum(0, 3)

@@ -321,11 +321,13 @@ def tile_informationinteraction_kernel(tc, x, conv_w_words, conv_w_scales, gamma
             quantise_x(1)
             multiply_gram(0, 0)
             keep_right(0, 0)
-            convolve(0, 0)
             turn_x(1, 0)
+            keep_flipped(1, 0)
+            convolve(0, 0)
+            turn_x(1, 1)
+            keep_flipped(1, 1)
             convolve(0, 1)
             convolve(0, 2)
-            keep_flipped(1, 0)
             y_statistics(0, 0)
             row_maximum(0, 0)
             softmax(0, 0)
@@ -334,10 +336,10 @@ def tile_informationinteraction_kernel(tc, x, conv_w_words, conv_w_scales, gamma
             y_statistics(0, 2)
             multiply_gram(0, 1)
             keep_right(0, 1)
+            turn_x(1, 2)
+            keep_flipped(1, 2)
             convolve(0, 3)
             convolve(1, 0)
-            turn_x(1, 1)
-            keep_flipped(1, 1)
             convolve(1, 1)
             row_maximum(0, 1)
             softmax(0, 1)
@@ -348,8 +350,6 @@ def tile_informationinteraction_kernel(tc, x, conv_w_words, conv_w_scales, gamma
             y_statistics(1, 1)
             multiply_gram(0, 2)
             keep_right(0, 2)
-            turn_x(1, 2)
-            keep_flipped(1, 2)
             convolve(1, 2)
             convolve(1, 3)
             row_maximum(0, 2)

from contextlib import ExitStack

import concourse.mybir as mybir
from concourse.masks import make_identity

F32 = mybir.dt.float32
BF16 = mybir.dt.bfloat16
I32 = mybir.dt.int32
U32 = mybir.dt.uint32
U8 = mybir.dt.uint8
FP8X4 = mybir.dt.float8_e4m3fn_x4
ACT = mybir.ActivationFunctionType
ALU = mybir.AluOpType
AXIS = mybir.AxisListType

P = 128
PACK = 4
IMAGES = 2
CHANNELS = 512
PIXELS = 768
COLUMNS = IMAGES * PIXELS
CH_TILES = CHANNELS // P
PAIR_TILES = PIXELS // (2 * P)
BANK = 512
COL_CHUNKS = COLUMNS // BANK
RUN = 4
EPS = 1e-5

FLOPS = 3 * 2 * IMAGES * CHANNELS * CHANNELS * PIXELS


def tile_informationinteraction_kernel(tc, x, conv_w_words, conv_w_scales, gamma, beta, out):
    nc = tc.nc
    x_img = x.rearrange("b c h w -> b c (h w)")
    out_img = out.rearrange("b c h w -> b c (h w)")

    with ExitStack() as ctx:
        keep = ctx.enter_context(tc.tile_pool(name="keep", bufs=1))
        work = ctx.enter_context(tc.tile_pool(name="work", bufs=4))
        late = ctx.enter_context(tc.tile_pool(name="late", bufs=2 * IMAGES * CH_TILES))
        flip_psum = ctx.enter_context(tc.psum_pool(name="flip_psum", bufs=2))
        gram_psum = ctx.enter_context(tc.psum_pool(name="gram_psum", bufs=3))
        mx_psum = ctx.enter_context(tc.psum_pool(name="mx_psum", bufs=3))

        x_quads = [keep.tile([P, PACK, PIXELS], BF16, name="x_quads%d" % b) for b in range(IMAGES)]
        w_codes = keep.tile([P, PACK * CHANNELS], U8, align_bytes=64)
        w_scales = keep.tile([P, CHANNELS], U8, align_bytes=64)
        nc.vector.memset(w_scales[:].bitcast(I32), 0)

        def load_quads(b, first, last):
            nc.sync.dma_start(
                out=x_quads[b][:, :, first:last], in_=x_img[b].rearrange("(p t) n -> p t n", t=PACK)[:, :, first:last]
            )

        load_quads(0, 0, BANK)
        load_quads(0, BANK, PIXELS)
        load_quads(1, 0, PIXELS)
        nc.sync.dma_start(
            out=w_codes[:].bitcast(I32),
            in_=conv_w_words[0].rearrange("p n t -> p (n t)").bitcast(I32),
        )
        for quadrant in range(4):
            nc.sync.dma_start(
                out=w_scales[32 * quadrant : 32 * quadrant + 4, :].bitcast(I32),
                in_=conv_w_scales[0, 4 * quadrant : 4 * quadrant + 4, :].bitcast(I32),
            )

        ident = keep.tile([P, P], BF16)
        make_identity(nc, ident[:])
        ident_words = keep.tile([P, P], F32)

        affine_rows = keep.tile([P, P], BF16)
        nc.vector.memset(affine_rows[:], 0.0)
        nc.scalar.dma_start(out=affine_rows[0:CH_TILES, :], in_=gamma.rearrange("(j p) -> j p", p=P))
        nc.scalar.dma_start(out=affine_rows[CH_TILES : 2 * CH_TILES, :], in_=beta.rearrange("(j p) -> j p", p=P))

        x_grouped = keep.tile([P, COLUMNS, PACK], BF16, align_bytes=64)
        x_codes = keep.tile([P, COLUMNS], U32, align_bytes=64)
        x_scales = keep.tile([P, COLUMNS], U8, align_bytes=64)

        def regroup(b, first, last, copy=nc.vector.tensor_copy):
            copy(
                out=x_grouped[:, b * PIXELS + first : b * PIXELS + last, :].rearrange("p (n i) t -> p n t i", i=RUN),
                in_=x_quads[b][:, :, first:last].rearrange("p t (n i) -> p n t i", i=RUN),
            )

        def quantise_x(k):
            cols = slice(k * BANK, (k + 1) * BANK)
            nc.vector.quantize_mx(
                out=x_codes[:, cols].bitcast(FP8X4),
                scales=x_scales[:, cols],
                in_=x_grouped[:, cols, :].rearrange("p n t -> p (n t)"),
            )

        x_flipped = keep.tile([P, IMAGES, PAIR_TILES, CHANNELS], F32)

        idle = keep.tile([P, BANK], BF16)
        nc.vector.memset(idle[:], 0.0)

        def warm_up(n):
            idle_ps = mx_psum.tile([P, BANK], F32, tag="mx")
            for i in range(n):
                nc.tensor.matmul(out=idle_ps[:], lhsT=idle[:, 0:P], rhs=idle[:], start=True, stop=True)

        flipped = {}

        def turn_x(b, i):
            pixels = slice(2 * P * i, 2 * P * (i + 1))
            if b == 0 and i == 2:
                x_ps = mx_psum.tile([P, PACK, P], F32, tag="mx")
            else:
                x_ps = flip_psum.tile([P, PACK, P], F32, tag="flip")
            for t in range(PACK):
                nc.tensor.transpose(x_ps[:, t, :], x_quads[b][:, t, pixels].bitcast(F32), ident_words[:])
            flipped[b, i] = x_ps

        def keep_flipped(b, i):
            nc.scalar.copy(
                out=x_flipped[:, b, i, :].rearrange("q (p t) -> q p t", t=PACK),
                in_=flipped[b, i][:].rearrange("q t p -> q p t"),
            )

        stats = keep.tile([P, CH_TILES, COL_CHUNKS, 6], F32)

        def multiply_y(y_ps, j, cols):
            nc.tensor.matmul_mx(
                out=y_ps,
                lhsT=w_codes[:, PACK * P * j : PACK * P * (j + 1)].bitcast(FP8X4),
                lhsT_scale=w_scales[:, P * j : P * (j + 1)],
                rhs=x_codes[:, cols].bitcast(FP8X4),
                rhs_scale=x_scales[:, cols],
                start=True,
                stop=True,
            )

        y_psum = {}

        def convolve(k, j):
            y_ps = mx_psum.tile([P, BANK], F32, tag="mx")
            multiply_y(y_ps[:], j, slice(k * BANK, (k + 1) * BANK))
            y_psum[k, j] = y_ps

        def y_statistics(k, j):
            nc.vector.bn_stats(out=stats[:, j, k, :], in_=y_psum[k, j][:])

        affine = keep.tile([P, 2 * CH_TILES], F32)
        mean_var = keep.tile([P, CH_TILES, 2], F32)
        var_eps = keep.tile([P, CH_TILES], F32)
        minus_half = keep.tile([P, CH_TILES], F32)
        rstd = keep.tile([P, CH_TILES], F32)
        inv = keep.tile([P, CH_TILES], F32)
        mean_inv = keep.tile([P, CH_TILES], F32)
        shift = keep.tile([P, CH_TILES], F32)
        nc.gpsimd.memset(minus_half[:], -0.5)

        def load_affine():
            affine_ps = flip_psum.tile([P, P], BF16, tag="flip")
            nc.tensor.transpose(affine_ps[:], affine_rows[:], ident[:])
            nc.scalar.copy(out=affine[:], in_=affine_ps[:, 0 : 2 * CH_TILES])

        def aggregate_statistics():
            for j in range(CH_TILES):
                nc.vector.bn_aggr(out=mean_var[:, j, :], in_=stats[:, j].rearrange("p k s -> p (k s)"))
            nc.gpsimd.tensor_scalar(out=var_eps[:], in0=mean_var[:, :, 1], scalar1=1.0, scalar2=EPS, op0=ALU.mult, op1=ALU.add)
            nc.gpsimd.tensor_tensor(out=rstd[:], in0=var_eps[:], in1=minus_half[:], op=ALU.pow)

        def fold_statistics():
            nc.gpsimd.tensor_tensor(out=inv[:], in0=affine[:, 0:CH_TILES], in1=rstd[:], op=ALU.mult)
            nc.gpsimd.tensor_tensor(out=mean_inv[:], in0=mean_var[:, :, 0], in1=inv[:], op=ALU.mult)
            nc.gpsimd.tensor_tensor(out=shift[:], in0=affine[:, CH_TILES : 2 * CH_TILES], in1=mean_inv[:], op=ALU.subtract)

        neg_max = keep.tile([P, IMAGES, CH_TILES], F32)
        row_sum = keep.tile([P, IMAGES, CH_TILES], F32)
        row_inv = keep.tile([P, IMAGES, CH_TILES], F32)
        att_codes = keep.tile([P, IMAGES, CHANNELS], U32, align_bytes=64)
        att_scales = keep.tile([P, IMAGES, CHANNELS], U8, align_bytes=64)
        gram = {}
        right_of_diagonal = {}
        expo = {}
        att = {}
        att_psum = {}
        att_grouped = {}

        def multiply_gram(b, j):
            rows = slice(P * j, P * (j + 1))
            g_ps = gram_psum.tile([P, CHANNELS], F32, tag="gram")
            gram[b, j] = g_ps
            for i in range(PAIR_TILES):
                halves = x_flipped[:, b, i, :].bitcast(BF16).rearrange("q (c e) -> q c e", e=2)
                for e in range(2):
                    nc.tensor.matmul(
                        out=g_ps[:, P * j :],
                        lhsT=halves[:, rows, e],
                        rhs=halves[:, P * j :, e],
                        start=(i == 0 and e == 0),
                        stop=(i == PAIR_TILES - 1 and e == 1),
                    )
            for earlier in range(j):
                nc.tensor.transpose(
                    g_ps[:, P * earlier : P * (earlier + 1)],
                    right_of_diagonal[b, earlier][:, P * (j - earlier - 1) : P * (j - earlier)],
                    ident_words[:],
                )

        def keep_right(b, j):
            if j + 1 < CH_TILES:
                g_ps = gram[b, j]
                kept = work.tile([P, CHANNELS - P * (j + 1)], F32, name="right_of_diagonal%d" % j)
                nc.scalar.copy(out=kept[:], in_=g_ps[:, P * (j + 1) :])
                right_of_diagonal[b, j] = kept

        def row_maximum(b, j):
            nc.vector.tensor_reduce(out=neg_max[:, b, j : j + 1], in_=gram[b, j][:], axis=AXIS.X, op=ALU.max, negate=True)

        def softmax(b, j):
            g_ps = gram[b, j]
            exponentials = work.tile([P, 2, P, 2], F32, name="exponentials")
            nc.scalar.activation(
                out=exponentials[:],
                in_=g_ps[:].rearrange("c (p u e) -> c u p e", u=2, e=2),
                func=ACT.Exp,
                bias=neg_max[:, b, j : j + 1],
                scale=1.0,
                accum_out=row_sum[:, b, j : j + 1],
            )
            expo[b, j] = exponentials

        def invert_sum(b, j):
            nc.vector.reciprocal(out=row_inv[:, b, j : j + 1], in_=row_sum[:, b, j : j + 1])

        def divide(b, j):
            divided = work.tile([P, 2, 2 * P], BF16, name="divided")
            nc.gpsimd.tensor_scalar(
                out=divided[:].rearrange("c u w -> c (u w)"),
                in0=expo[b, j][:].rearrange("c u p e -> c (u p e)"),
                scalar1=row_inv[:, b, j : j + 1],
                scalar2=0.0,
                op0=ALU.mult,
                op1=ALU.add,
            )
            att[b, j] = divided

        def turn_att(b, j):
            att_ps = flip_psum.tile([P, 2, P], F32, tag="flip")
            for u in range(2):
                nc.tensor.transpose(att_ps[:, u, :], att[b, j][:, u, :].bitcast(F32), ident_words[:])
            att_psum[b, j] = att_ps

        def group_att(b, j):
            grouped = work.tile([P, P, 2], F32, align_bytes=64, name="att_grouped")
            nc.scalar.copy(out=grouped[:], in_=att_psum[b, j][:].rearrange("p u c -> p c u"))
            att_grouped[b, j] = grouped

        def quantise_att(b, j):
            rows = slice(P * j, P * (j + 1))
            nc.vector.quantize_mx(
                out=att_codes[:, b, rows].bitcast(FP8X4),
                scales=att_scales[:, b, rows],
                in_=att_grouped[b, j][:].rearrange("p c u -> p (c u)").bitcast(BF16),
            )

        y_act = {}

        y_psum2 = {}

        def repeat_y(b, j, first, width):
            y_ps = mx_psum.tile([P, BANK], F32, tag="mx")
            multiply_y(y_ps[:, 0:width], j, slice(b * PIXELS + first, b * PIXELS + first + width))
            y_psum2[b, j, first] = y_ps

        def activate_y(b, j, first, width):
            activated = late.tile([P, BANK], F32, name="activated")
            nc.scalar.activation(
                out=activated[:, 0:width],
                in_=y_psum2[b, j, first][:, 0:width],
                func=ACT.Relu,
                bias=shift[:, j : j + 1],
                scale=inv[:, j : j + 1],
            )
            y_act[b, j, first] = activated

        sp_psum = {}

        def multiply_sp(b, j, first, width):
            rows = slice(P * j, P * (j + 1))
            cols = slice(b * PIXELS + first, b * PIXELS + first + width)
            sp_ps = gram_psum.tile([P, BANK], F32, tag="gram")
            nc.tensor.matmul_mx(
                out=sp_ps[:, 0:width],
                lhsT=att_codes[:, b, rows].bitcast(FP8X4),
                lhsT_scale=att_scales[:, b, rows],
                rhs=x_codes[:, cols].bitcast(FP8X4),
                rhs_scale=x_scales[:, cols],
                start=True,
                stop=True,
            )
            sp_psum[b, j, first] = sp_ps

        def emit(b, j, first, width):
            rows = slice(P * j, P * (j + 1))
            result = late.tile([P, BANK], F32, name="result")
            nc.vector.tensor_tensor(out=result[:, 0:width], in0=y_act[b, j, first][:, 0:width], in1=sp_psum[b, j, first][:, 0:width], op=ALU.add)
            nc.sync.dma_start(out=out_img[b, rows, first : first + width], in_=result[:, 0:width])

        pieces = [(0, BANK), (BANK, PIXELS - BANK)]
        with tc.manual_schedule():
            nc.vector.tensor_copy(out=ident_words[:], in_=ident[:])
            warm_up(5)
            regroup(0, 0, BANK)
            regroup(0, BANK, PIXELS)
            quantise_x(0)
            turn_x(0, 0)
            keep_flipped(0, 0)
            turn_x(0, 1)
            keep_flipped(0, 1)
            turn_x(0, 2)
            keep_flipped(0, 2)
            regroup(1, BANK, PIXELS, nc.scalar.copy)
            regroup(1, 0, PIXELS - BANK)
            regroup(1, PIXELS - BANK, BANK)
            quantise_x(1)
            multiply_gram(0, 0)
            keep_right(0, 0)
            turn_x(1, 0)
            keep_flipped(1, 0)
            convolve(0, 0)
            turn_x(1, 1)
            keep_flipped(1, 1)
            convolve(0, 1)
            convolve(0, 2)
            y_statistics(0, 0)
            row_maximum(0, 0)
            softmax(0, 0)
            quantise_x(2)
            y_statistics(0, 1)
            y_statistics(0, 2)
            multiply_gram(0, 1)
            keep_right(0, 1)
            turn_x(1, 2)
            keep_flipped(1, 2)
            convolve(0, 3)
            convolve(1, 0)
            convolve(1, 1)
            row_maximum(0, 1)
            softmax(0, 1)
            invert_sum(0, 0)
            divide(0, 0)
            y_statistics(0, 3)
            y_statistics(1, 0)
            y_statistics(1, 1)
            multiply_gram(0, 2)
            keep_right(0, 2)
            convolve(1, 2)
            convolve(1, 3)
            row_maximum(0, 2)
            softmax(0, 2)
            invert_sum(0, 1)
            divide(0, 1)
            load_affine()
            y_statistics(1, 2)
            y_statistics(1, 3)
            multiply_gram(0, 3)
            convolve(2, 0)
            convolve(2, 1)
            row_maximum(0, 3)
            softmax(0, 3)
            invert_sum(0, 2)
            divide(0, 2)
            y_statistics(2, 0)
            y_statistics(2, 1)
            multiply_gram(1, 0)
            keep_right(1, 0)
            convolve(2, 2)
            convolve(2, 3)
            turn_att(0, 0)
            group_att(0, 0)
            y_statistics(2, 2)
            row_maximum(1, 0)
            softmax(1, 0)
            invert_sum(0, 3)
            divide(0, 3)
            y_statistics(2, 3)
            aggregate_statistics()
            fold_statistics()
            multiply_gram(1, 1)
            keep_right(1, 1)
            turn_att(0, 1)
            group_att(0, 1)
            row_maximum(1, 1)
            softmax(1, 1)
            invert_sum(1, 0)
            divide(1, 0)
            quantise_att(0, 0)
            quantise_att(0, 1)
            multiply_gram(1, 2)
            keep_right(1, 2)
            turn_att(0, 2)
            group_att(0, 2)
            row_maximum(1, 2)
            softmax(1, 2)
            invert_sum(1, 1)
            divide(1, 1)
            quantise_att(0, 2)
            repeat_y(0, 0, 0, BANK)
            repeat_y(0, 0, BANK, PIXELS - BANK)
            multiply_gram(1, 3)
            turn_att(0, 3)
            group_att(0, 3)
            activate_y(0, 0, 0, BANK)
            activate_y(0, 0, BANK, PIXELS - BANK)
            row_maximum(1, 3)
            softmax(1, 3)
            invert_sum(1, 2)
            divide(1, 2)
            quantise_att(0, 3)
            multiply_sp(0, 0, 0, BANK)
            multiply_sp(0, 0, BANK, PIXELS - BANK)
            repeat_y(0, 1, 0, BANK)
            repeat_y(0, 1, BANK, PIXELS - BANK)
            emit(0, 0, 0, BANK)
            turn_att(1, 0)
            group_att(1, 0)
            activate_y(0, 1, 0, BANK)
            emit(0, 0, BANK, PIXELS - BANK)
            activate_y(0, 1, BANK, PIXELS - BANK)
            multiply_sp(0, 1, 0, BANK)
            multiply_sp(0, 1, BANK, PIXELS - BANK)
            invert_sum(1, 3)
            divide(1, 3)
            repeat_y(0, 2, 0, BANK)
            repeat_y(0, 2, BANK, PIXELS - BANK)
            emit(0, 1, 0, BANK)
            activate_y(0, 2, 0, BANK)
            emit(0, 1, BANK, PIXELS - BANK)
            turn_att(1, 1)
            group_att(1, 1)
            quantise_att(1, 0)
            activate_y(0, 2, BANK, PIXELS - BANK)
            multiply_sp(0, 2, 0, BANK)
            multiply_sp(0, 2, BANK, PIXELS - BANK)
            repeat_y(0, 3, 0, BANK)
            repeat_y(0, 3, BANK, PIXELS - BANK)
            emit(0, 2, 0, BANK)
            activate_y(0, 3, 0, BANK)
            emit(0, 2, BANK, PIXELS - BANK)
            turn_att(1, 2)
            group_att(1, 2)
            quantise_att(1, 1)
            activate_y(0, 3, BANK, PIXELS - BANK)
            multiply_sp(0, 3, 0, BANK)
            multiply_sp(0, 3, BANK, PIXELS - BANK)
            repeat_y(1, 0, 0, BANK)
            repeat_y(1, 0, BANK, PIXELS - BANK)
            emit(0, 3, 0, BANK)
            activate_y(1, 0, 0, BANK)
            emit(0, 3, BANK, PIXELS - BANK)
            turn_att(1, 3)
            group_att(1, 3)
            quantise_att(1, 2)
            activate_y(1, 0, BANK, PIXELS - BANK)
            multiply_sp(1, 0, 0, BANK)
            multiply_sp(1, 0, BANK, PIXELS - BANK)
            repeat_y(1, 1, 0, BANK)
            repeat_y(1, 1, BANK, PIXELS - BANK)
            emit(1, 0, 0, BANK)
            activate_y(1, 1, 0, BANK)
            emit(1, 0, BANK, PIXELS - BANK)
            quantise_att(1, 3)
            activate_y(1, 1, BANK, PIXELS - BANK)
            multiply_sp(1, 1, 0, BANK)
            multiply_sp(1, 1, BANK, PIXELS - BANK)
            repeat_y(1, 2, 0, BANK)
            repeat_y(1, 2, BANK, PIXELS - BANK)
            emit(1, 1, 0, BANK)
            activate_y(1, 2, 0, BANK)
            emit(1, 1, BANK, PIXELS - BANK)
            activate_y(1, 2, BANK, PIXELS - BANK)
            multiply_sp(1, 2, 0, BANK)
            multiply_sp(1, 2, BANK, PIXELS - BANK)
            repeat_y(1, 3, 0, BANK)
            repeat_y(1, 3, BANK, PIXELS - BANK)
            emit(1, 2, 0, BANK)
            activate_y(1, 3, 0, BANK)
            emit(1, 2, BANK, PIXELS - BANK)
            activate_y(1, 3, BANK, PIXELS - BANK)
            multiply_sp(1, 3, 0, BANK)
            multiply_sp(1, 3, BANK, PIXELS - BANK)
            emit(1, 3, 0, BANK)
            emit(1, 3, BANK, PIXELS - BANK)
